import numpy as np
import ml_dtypes


def mxq(x, axis, fmt="e4m3"):
    dtype, down = {"e4m3": (ml_dtypes.float8_e4m3fn, 7), "e5m2": (ml_dtypes.float8_e5m2, 14)}[fmt]
    v = np.moveaxis(np.asarray(x, np.float32).astype(ml_dtypes.bfloat16).astype(np.float64), axis, -1)
    blocks = v.reshape(v.shape[:-1] + (-1, 32))
    amax = np.abs(blocks).max(-1, keepdims=True)
    byte = np.maximum(np.where(amax > 0, np.frexp(amax)[1] - 1 + 127, 0) - down, 1)
    scale = np.exp2(byte - 127.0)
    codes = (blocks / scale).astype(np.float32).astype(dtype).astype(np.float64)
    return np.moveaxis((codes * scale).reshape(v.shape), -1, axis)


WIDE = False


def mx_kscale(k):
    if not WIDE:
        return np.ones(k)
    levels = np.array([10, -10, 5, -5, 0])
    a = np.random.permutation(np.resize(levels, k // 512 * 4)).reshape(k // 512, 4)
    idx = np.arange(k)
    return np.exp2(a[idx // 512, idx % 128 // 32])


BF16 = ml_dtypes.bfloat16


def bf(x):
    return np.asarray(x, np.float32).astype(BF16)


def f64(x):
    return np.asarray(x).astype(np.float64)


B, N, D = 4, 512, 128


def sigmoid(u):
    return 1.0 / (1.0 + np.exp(-u))


def setup_inputs():
    a = np.log(mx_kscale(N))
    return {"q": bf(np.random.standard_normal((B, N, D))),
            "k": bf(np.random.standard_normal((B, N, D)) - a[None, :, None]),
            "v": bf(np.random.standard_normal((B, N, D)) * 0.125 * np.sqrt(N)),
            "bias": bf(np.random.standard_normal((N, N)) + a[None, :])}


def reference(q, k, v, bias):
    q, k, v, bias = f64(q), f64(k), f64(v), f64(bias)
    mb = bias.max(axis=1, keepdims=True)
    mk = k.max(axis=1, keepdims=True)
    eb = np.exp(bias - mb)
    ek = np.exp(k - mk)
    ebq = mxq(eb, 1, "e4m3")
    num = ebq @ mxq(ek * v, 1, "e4m3")
    den = ebq @ mxq(ek, 1, "e4m3")
    return sigmoid(q) * (num / den)

@@ -1,0 +1,174 @@
+import concourse.mybir as mybir
+from concourse.masks import make_identity
+
+FP8X4 = mybir.dt.float8_e4m3fn_x4
+BF16 = mybir.dt.bfloat16
+F32 = mybir.dt.float32
+U32 = mybir.dt.uint32
+U8 = mybir.dt.uint8
+ACT = mybir.ActivationFunctionType
+ALU = mybir.AluOpType
+AXIS = mybir.AxisListType
+
+P = 128
+PACK = 4
+B, N, D = 4, 512, 128
+ROWS = N // P
+FLOPS = 2 * 2 * B * N * N * D
+
+
+def tile_modelnew_s_kernel(tc, q, k, v, bias, out):
+    nc = tc.nc
+    with tc.tile_pool(name="sbuf", bufs=1) as sbuf, tc.psum_pool(name="psum", bufs=1) as psum:
+        k_sb = sbuf.tile([P, B, PACK, D], BF16)
+        v_sb = sbuf.tile([P, B, PACK, D], BF16)
+        q_sb = sbuf.tile([P, B, ROWS, D], BF16)
+        bias_sb = sbuf.tile([P, ROWS, N], BF16)
+        k_view = k.rearrange("b (c t) d -> c b t d", t=PACK)
+        v_view = v.rearrange("b (c t) d -> c b t d", t=PACK)
+        q_view = q.rearrange("b (p s) d -> p b s d", s=ROWS)
+        bias_view = bias.rearrange("(p s) j -> p s j", s=ROWS)
+        out_view = out.rearrange("b (p s) d -> p s b d", s=ROWS)
+        nc.sync.dma_start(out=k_sb[:], in_=k_view)
+        nc.sync.dma_start(out=bias_sb[:, 0:2, :], in_=bias_view[:, 0:2, :])
+        nc.sync.dma_start(out=bias_sb[:, 2:4, :], in_=bias_view[:, 2:4, :])
+        nc.sync.dma_start(out=v_sb[:], in_=v_view)
+        nc.sync.dma_start(out=q_sb[:], in_=q_view)
+
+        ident = sbuf.tile([P, P], BF16)
+        make_identity(nc, ident[:])
+
+        k_max2 = sbuf.tile([P, B, 2, D], BF16)
+        k_max1 = sbuf.tile([P, B, D], BF16)
+        nc.vector.tensor_tensor(
+            out=k_max2[:], in0=k_sb[:, :, 0:2, :], in1=k_sb[:, :, 2:4, :], op=ALU.max
+        )
+        nc.vector.tensor_tensor(
+            out=k_max1[:], in0=k_max2[:, :, 0, :], in1=k_max2[:, :, 1, :], op=ALU.max
+        )
+        k_maxT = psum.tile([P, B, P], BF16, tag="bank4")
+        for b in range(B):
+            nc.tensor.transpose(k_maxT[:, b, :], k_max1[:, b, :], ident[:])
+        mk = sbuf.tile([P, B], BF16)
+        with nc.allow_low_precision(reason="a maximum of bfloat16 values is a bfloat16 value"):
+            nc.vector.tensor_reduce(out=mk[:], in_=k_maxT[:], axis=AXIS.X, op=ALU.max)
+        mk_all = psum.tile([P, B, D], F32, tag="bank5")
+        for b in range(B):
+            nc.tensor.matmul(
+                out=mk_all[:, b, :],
+                lhsT=mk[:, b : b + 1].to_broadcast([P, P]),
+                rhs=ident[:],
+                start=True,
+                stop=True,
+            )
+
+        neg_mb = sbuf.tile([P, ROWS], F32)
+        eb_sb = sbuf.tile([P, ROWS, PACK, P], BF16)
+        eb_grouped = sbuf.tile([P, ROWS, P, PACK], BF16, align_bytes=64)
+        for s in range(ROWS):
+            nc.vector.tensor_reduce(
+                out=neg_mb[:, s : s + 1], in_=bias_sb[:, s, :], axis=AXIS.X, op=ALU.max, negate=True
+            )
+            nc.scalar.activation(
+                out=eb_sb[:, s, :, :],
+                in_=bias_sb[:, s, :].rearrange("p (c t) -> p t c", t=PACK),
+                func=ACT.Exp,
+                bias=neg_mb[:, s : s + 1],
+                scale=1.0,
+            )
+            ebT = psum.tile([P, PACK, P], BF16, tag="bank%d" % s, name="ebT%d" % s)
+            for t in range(PACK):
+                nc.tensor.transpose(ebT[:, t, :], eb_sb[:, s, t, :], ident[:])
+            nc.scalar.copy(out=eb_grouped[:, s, :, :], in_=ebT[:].rearrange("c t p -> c p t"))
+
+        k_diff = sbuf.tile([P, B, D, PACK], F32)
+        ek_f32 = sbuf.tile([P, B, D, PACK], F32)
+        ek_grouped = sbuf.tile([P, B, D, PACK], BF16, align_bytes=64)
+        ekv_grouped = sbuf.tile([P, B, D, PACK], BF16, align_bytes=64)
+        for b in range(B):
+            nc.vector.tensor_tensor(
+                out=k_diff[:, b],
+                in0=k_sb[:, b].rearrange("c t d -> c d t"),
+                in1=mk_all[:, b, :].unsqueeze(2).to_broadcast([P, D, PACK]),
+                op=ALU.subtract,
+            )
+            nc.scalar.activation(out=ek_f32[:, b], in_=k_diff[:, b], func=ACT.Exp)
+            nc.vector.tensor_copy(out=ek_grouped[:, b], in_=ek_f32[:, b])
+
+        eb_codes = sbuf.tile([P, ROWS * P], U32, align_bytes=64)
+        eb_scales = sbuf.tile([P, ROWS * P], U8, align_bytes=64)
+        ek_codes = sbuf.tile([P, B * D], U32, align_bytes=64)
+        ek_scales = sbuf.tile([P, B * D], U8, align_bytes=64)
+        ekv_codes = sbuf.tile([P, B * D], U32, align_bytes=64)
+        ekv_scales = sbuf.tile([P, B * D], U8, align_bytes=64)
+        nc.vector.quantize_mx(
+            out=eb_codes[:].bitcast(FP8X4),
+            scales=eb_scales[:],
+            in_=eb_grouped[:].rearrange("c s p t -> c (s p t)"),
+        )
+        nc.vector.quantize_mx(
+            out=ek_codes[:].bitcast(FP8X4),
+            scales=ek_scales[:],
+            in_=ek_grouped[:].rearrange("c b d t -> c (b d t)"),
+        )
+        den = []
+        for s in range(ROWS):
+            den_s = psum.tile([P, B * D], F32, tag="bank%d" % s, name="den%d" % s)
+            nc.tensor.matmul_mx(
+                out=den_s[:],
+                lhsT=eb_codes[:, s * P : (s + 1) * P].bitcast(FP8X4),
+                lhsT_scale=eb_scales[:, s * P : (s + 1) * P],
+                rhs=ek_codes[:].bitcast(FP8X4),
+                rhs_scale=ek_scales[:],
+                start=True,
+                stop=True,
+            )
+            den.append(den_s)
+
+        e_sb = sbuf.tile([P, ROWS, B, D], F32)
+        w_sb = sbuf.tile([P, ROWS, B * D], F32)
+        for s in range(ROWS):
+            nc.scalar.activation(out=e_sb[:, s], in_=q_sb[:, :, s, :], func=ACT.Exp, scale=-1.0)
+        for s in range(ROWS):
+            nc.vector.scalar_tensor_tensor(
+                out=w_sb[:, s, :],
+                in0=e_sb[:, s].rearrange("p b d -> p (b d)"),
+                scalar=1.0,
+                in1=den[s][:],
+                op0=ALU.add,
+                op1=ALU.mult,
+            )
+
+        for b in range(B):
+            nc.vector.tensor_tensor(
+                out=ekv_grouped[:, b],
+                in0=ek_f32[:, b],
+                in1=v_sb[:, b].rearrange("c t d -> c d t"),
+                op=ALU.mult,
+            )
+        nc.vector.quantize_mx(
+            out=ekv_codes[:].bitcast(FP8X4),
+            scales=ekv_scales[:],
+            in_=ekv_grouped[:].rearrange("c b d t -> c (b d t)"),
+        )
+
+        rsqrt_w = sbuf.tile([P, ROWS, B * D], F32)
+        recip_w = sbuf.tile([P, ROWS, B * D], F32)
+        o_sb = sbuf.tile([P, ROWS, B * D], F32)
+        for s in range(ROWS):
+            num_s = psum.tile([P, B * D], F32, tag="bank%d" % (4 + s), name="num%d" % s)
+            nc.tensor.matmul_mx(
+                out=num_s[:],
+                lhsT=eb_codes[:, s * P : (s + 1) * P].bitcast(FP8X4),
+                lhsT_scale=eb_scales[:, s * P : (s + 1) * P],
+                rhs=ekv_codes[:].bitcast(FP8X4),
+                rhs_scale=ekv_scales[:],
+                start=True,
+                stop=True,
+            )
+            nc.scalar.activation(out=rsqrt_w[:, s, :], in_=w_sb[:, s, :], func=ACT.Abs_reciprocal_sqrt)
+            nc.scalar.activation(out=recip_w[:, s, :], in_=rsqrt_w[:, s, :], func=ACT.Square)
+            nc.vector.tensor_tensor(out=o_sb[:, s, :], in0=num_s[:], in1=recip_w[:, s, :], op=ALU.mult)
+            nc.sync.dma_start(
+                out=out_view[:, s], in_=o_sb[:, s, :].rearrange("p (b d) -> p b d", b=B)
+            )

@@ -19,7 +19,11 @@ FLOPS = 2 * 2 * B * N * N * D
 
 def tile_modelnew_s_kernel(tc, q, k, v, bias, out):
     nc = tc.nc
-    with tc.tile_pool(name="sbuf", bufs=1) as sbuf, tc.psum_pool(name="psum", bufs=1) as psum:
+    with (
+        tc.tile_pool(name="sbuf", bufs=1) as sbuf,
+        tc.psum_pool(name="psum", bufs=1) as psum,
+        tc.manual_schedule(),
+    ):
         k_sb = sbuf.tile([P, B, PACK, D], BF16)
         v_sb = sbuf.tile([P, B, PACK, D], BF16)
         q_sb = sbuf.tile([P, B, ROWS, D], BF16)
@@ -29,30 +33,133 @@ def tile_modelnew_s_kernel(tc, q, k, v, bias, out):
         q_view = q.rearrange("b (p s) d -> p b s d", s=ROWS)
         bias_view = bias.rearrange("(p s) j -> p s j", s=ROWS)
         out_view = out.rearrange("b (p s) d -> p s b d", s=ROWS)
-        nc.sync.dma_start(out=k_sb[:], in_=k_view)
-        nc.sync.dma_start(out=bias_sb[:, 0:2, :], in_=bias_view[:, 0:2, :])
-        nc.sync.dma_start(out=bias_sb[:, 2:4, :], in_=bias_view[:, 2:4, :])
-        nc.sync.dma_start(out=v_sb[:], in_=v_view)
-        nc.sync.dma_start(out=q_sb[:], in_=q_view)
 
         ident = sbuf.tile([P, P], BF16)
-        make_identity(nc, ident[:])
+        one = sbuf.tile([P, 1], F32)
+        warm_exp = sbuf.tile([P, 1], F32)
+        warm_rsqrt = sbuf.tile([P, 1], F32)
+
+        neg_mb = sbuf.tile([P, ROWS], F32)
+        eb_sb = sbuf.tile([P, ROWS, PACK, P], BF16)
+        eb_grouped = sbuf.tile([P, ROWS, P, PACK], BF16, align_bytes=64)
+        ebT = [
+            psum.tile([P, PACK, P], BF16, tag="bank%d" % s, name="ebT%d" % s) for s in range(ROWS)
+        ]
 
         k_max2 = sbuf.tile([P, B, 2, D], BF16)
         k_max1 = sbuf.tile([P, B, D], BF16)
+        k_maxT = psum.tile([P, B, P], BF16, tag="bank4")
+        mk = sbuf.tile([P, B], BF16)
+        mk_all = psum.tile([P, B, D], F32, tag="bank5")
+        k_diff = sbuf.tile([P, B, D, PACK], F32)
+        ek_f32 = sbuf.tile([P, B, D, PACK], F32)
+        ek_grouped = sbuf.tile([P, B, D, PACK], BF16, align_bytes=64)
+        ekv_grouped = sbuf.tile([P, B, D, PACK], BF16, align_bytes=64)
+
+        eb_codes = sbuf.tile([P, ROWS * P], U32, align_bytes=64)
+        eb_scales = sbuf.tile([P, ROWS * P], U8, align_bytes=64)
+        ek_codes = sbuf.tile([P, B * D], U32, align_bytes=64)
+        ek_scales = sbuf.tile([P, B * D], U8, align_bytes=64)
+        ekv_codes = sbuf.tile([P, B * D], U32, align_bytes=64)
+        ekv_scales = sbuf.tile([P, B * D], U8, align_bytes=64)
+
+        e_sb = sbuf.tile([P, ROWS, B, D], F32)
+        w_sb = sbuf.tile([P, ROWS, B * D], F32)
+        rsqrt_w = sbuf.tile([P, ROWS, B * D], F32)
+        recip_w = sbuf.tile([P, ROWS, B * D], F32)
+        o_sb = sbuf.tile([P, ROWS, B * D], F32)
+
+        def row_max(s):
+            nc.vector.tensor_reduce(
+                out=neg_mb[:, s : s + 1], in_=bias_sb[:, s, :], axis=AXIS.X, op=ALU.max, negate=True
+            )
+
+        def row_exp(s):
+            nc.scalar.activation(
+                out=eb_sb[:, s, :, :],
+                in_=bias_sb[:, s, :].rearrange("p (c t) -> p t c", t=PACK),
+                func=ACT.Exp,
+                bias=neg_mb[:, s : s + 1],
+                scale=1.0,
+            )
+
+        def row_transpose(s):
+            for t in range(PACK):
+                nc.tensor.transpose(ebT[s][:, t, :], eb_sb[:, s, t, :], ident[:])
+
+        def row_copy(engine_copy, s):
+            engine_copy(out=eb_grouped[:, s], in_=ebT[s][:].rearrange("c t p -> c p t"))
+
+        def gate_exp(s):
+            nc.scalar.activation(out=e_sb[:, s], in_=q_sb[:, :, s, :], func=ACT.Exp, scale=-1.0)
+
+        def k_subtract(b):
+            nc.vector.tensor_tensor(
+                out=k_diff[:, b],
+                in0=k_sb[:, b].rearrange("c t d -> c d t"),
+                in1=mk_all[:, b, :].unsqueeze(2).to_broadcast([P, D, PACK]),
+                op=ALU.subtract,
+            )
+
+        def k_exp(b):
+            nc.scalar.activation(out=ek_f32[:, b], in_=k_diff[:, b], func=ACT.Exp)
+
+        def ek_round(b):
+            nc.vector.tensor_copy(out=ek_grouped[:, b], in_=ek_f32[:, b])
+
+        def ek_times_v(b):
+            nc.vector.tensor_tensor(
+                out=ekv_grouped[:, b],
+                in0=ek_f32[:, b],
+                in1=v_sb[:, b].rearrange("c t d -> c d t"),
+                op=ALU.mult,
+            )
+
+        def quantise(codes, scales, grouped):
+            nc.vector.quantize_mx(out=codes[:].bitcast(FP8X4), scales=scales[:], in_=grouped)
+
+        def mx_product(acc, s, codes, scales):
+            nc.tensor.matmul_mx(
+                out=acc[:],
+                lhsT=eb_codes[:, s * P : (s + 1) * P].bitcast(FP8X4),
+                lhsT_scale=eb_scales[:, s * P : (s + 1) * P],
+                rhs=codes[:].bitcast(FP8X4),
+                rhs_scale=scales[:],
+                start=True,
+                stop=True,
+            )
+
+        nc.sync.dma_start(out=bias_sb[:, 0:2, :], in_=bias_view[:, 0:2, :])
+        nc.sync.dma_start(out=k_sb[:], in_=k_view)
+        nc.sync.dma_start(out=q_sb[:], in_=q_view)
+        nc.sync.dma_start(out=bias_sb[:, 2:4, :], in_=bias_view[:, 2:4, :])
+        nc.sync.dma_start(out=v_sb[:], in_=v_view)
+
+        make_identity(nc, ident[:])
+        nc.vector.memset(one[:], 1.0)
+        nc.scalar.activation(out=warm_exp[:], in_=one[:], func=ACT.Exp)
+
+        row_max(0)
+        row_max(1)
+        row_exp(0)
+        row_exp(1)
+        row_transpose(0)
         nc.vector.tensor_tensor(
             out=k_max2[:], in0=k_sb[:, :, 0:2, :], in1=k_sb[:, :, 2:4, :], op=ALU.max
         )
         nc.vector.tensor_tensor(
             out=k_max1[:], in0=k_max2[:, :, 0, :], in1=k_max2[:, :, 1, :], op=ALU.max
         )
-        k_maxT = psum.tile([P, B, P], BF16, tag="bank4")
         for b in range(B):
             nc.tensor.transpose(k_maxT[:, b, :], k_max1[:, b, :], ident[:])
-        mk = sbuf.tile([P, B], BF16)
+        row_transpose(1)
+        for s in range(ROWS - 1):
+            gate_exp(s)
+
+        row_max(2)
+        row_max(3)
         with nc.allow_low_precision(reason="a maximum of bfloat16 values is a bfloat16 value"):
             nc.vector.tensor_reduce(out=mk[:], in_=k_maxT[:], axis=AXIS.X, op=ALU.max)
-        mk_all = psum.tile([P, B, D], F32, tag="bank5")
         for b in range(B):
             nc.tensor.matmul(
                 out=mk_all[:, b, :],
@@ -61,75 +168,39 @@ def tile_modelnew_s_kernel(tc, q, k, v, bias, out):
                 start=True,
                 stop=True,
             )
+        row_copy(nc.vector.tensor_copy, 0)
+        row_copy(nc.scalar.copy, 1)
+        row_exp(2)
+        row_exp(3)
+        row_transpose(2)
+        row_transpose(3)
 
-        neg_mb = sbuf.tile([P, ROWS], F32)
-        eb_sb = sbuf.tile([P, ROWS, PACK, P], BF16)
-        eb_grouped = sbuf.tile([P, ROWS, P, PACK], BF16, align_bytes=64)
-        for s in range(ROWS):
-            nc.vector.tensor_reduce(
-                out=neg_mb[:, s : s + 1], in_=bias_sb[:, s, :], axis=AXIS.X, op=ALU.max, negate=True
-            )
-            nc.scalar.activation(
-                out=eb_sb[:, s, :, :],
-                in_=bias_sb[:, s, :].rearrange("p (c t) -> p t c", t=PACK),
-                func=ACT.Exp,
-                bias=neg_mb[:, s : s + 1],
-                scale=1.0,
-            )
-            ebT = psum.tile([P, PACK, P], BF16, tag="bank%d" % s, name="ebT%d" % s)
-            for t in range(PACK):
-                nc.tensor.transpose(ebT[:, t, :], eb_sb[:, s, t, :], ident[:])
-            nc.scalar.copy(out=eb_grouped[:, s, :, :], in_=ebT[:].rearrange("c t p -> c p t"))
-
-        k_diff = sbuf.tile([P, B, D, PACK], F32)
-        ek_f32 = sbuf.tile([P, B, D, PACK], F32)
-        ek_grouped = sbuf.tile([P, B, D, PACK], BF16, align_bytes=64)
-        ekv_grouped = sbuf.tile([P, B, D, PACK], BF16, align_bytes=64)
         for b in range(B):
-            nc.vector.tensor_tensor(
-                out=k_diff[:, b],
-                in0=k_sb[:, b].rearrange("c t d -> c d t"),
-                in1=mk_all[:, b, :].unsqueeze(2).to_broadcast([P, D, PACK]),
-                op=ALU.subtract,
-            )
-            nc.scalar.activation(out=ek_f32[:, b], in_=k_diff[:, b], func=ACT.Exp)
-            nc.vector.tensor_copy(out=ek_grouped[:, b], in_=ek_f32[:, b])
+            k_subtract(b)
+            k_exp(b)
+            if b + 2 < ROWS:
+                row_copy(nc.scalar.copy, b + 2)
+        gate_exp(ROWS - 1)
+        nc.scalar.activation(out=warm_rsqrt[:], in_=one[:], func=ACT.Abs_reciprocal_sqrt)
 
-        eb_codes = sbuf.tile([P, ROWS * P], U32, align_bytes=64)
-        eb_scales = sbuf.tile([P, ROWS * P], U8, align_bytes=64)
-        ek_codes = sbuf.tile([P, B * D], U32, align_bytes=64)
-        ek_scales = sbuf.tile([P, B * D], U8, align_bytes=64)
-        ekv_codes = sbuf.tile([P, B * D], U32, align_bytes=64)
-        ekv_scales = sbuf.tile([P, B * D], U8, align_bytes=64)
-        nc.vector.quantize_mx(
-            out=eb_codes[:].bitcast(FP8X4),
-            scales=eb_scales[:],
-            in_=eb_grouped[:].rearrange("c s p t -> c (s p t)"),
-        )
-        nc.vector.quantize_mx(
-            out=ek_codes[:].bitcast(FP8X4),
-            scales=ek_scales[:],
-            in_=ek_grouped[:].rearrange("c b d t -> c (b d t)"),
-        )
-        den = []
+        ek_round(0)
+        ek_round(1)
+        ek_times_v(0)
+        quantise(eb_codes, eb_scales, eb_grouped[:].rearrange("c s p t -> c (s p t)"))
+        ek_round(2)
+        ek_round(3)
+        quantise(ek_codes, ek_scales, ek_grouped[:].rearrange("c b d t -> c (b d t)"))
+        den = [
+            psum.tile([P, B * D], F32, tag="bank%d" % s, name="den%d" % s) for s in range(ROWS)
+        ]
         for s in range(ROWS):
-            den_s = psum.tile([P, B * D], F32, tag="bank%d" % s, name="den%d" % s)
-            nc.tensor.matmul_mx(
-                out=den_s[:],
-                lhsT=eb_codes[:, s * P : (s + 1) * P].bitcast(FP8X4),
-                lhsT_scale=eb_scales[:, s * P : (s + 1) * P],
-                rhs=ek_codes[:].bitcast(FP8X4),
-                rhs_scale=ek_scales[:],
-                start=True,
-                stop=True,
-            )
-            den.append(den_s)
+            mx_product(den[s], s, ek_codes, ek_scales)
 
-        e_sb = sbuf.tile([P, ROWS, B, D], F32)
-        w_sb = sbuf.tile([P, ROWS, B * D], F32)
         for s in range(ROWS):
-            nc.scalar.activation(out=e_sb[:, s], in_=q_sb[:, :, s, :], func=ACT.Exp, scale=-1.0)
-        for s in range(ROWS):
+            if s + 1 < B:
+                ek_times_v(s + 1)
+            else:
+                quantise(ekv_codes, ekv_scales, ekv_grouped[:].rearrange("c b d t -> c (b d t)"))
             nc.vector.scalar_tensor_tensor(
                 out=w_sb[:, s, :],
                 in0=e_sb[:, s].rearrange("p b d -> p (b d)"),
@@ -139,36 +210,16 @@ def tile_modelnew_s_kernel(tc, q, k, v, bias, out):
                 op1=ALU.mult,
             )
 
-        for b in range(B):
-            nc.vector.tensor_tensor(
-                out=ekv_grouped[:, b],
-                in0=ek_f32[:, b],
-                in1=v_sb[:, b].rearrange("c t d -> c d t"),
-                op=ALU.mult,
-            )
-        nc.vector.quantize_mx(
-            out=ekv_codes[:].bitcast(FP8X4),
-            scales=ekv_scales[:],
-            in_=ekv_grouped[:].rearrange("c b d t -> c (b d t)"),
-        )
-
-        rsqrt_w = sbuf.tile([P, ROWS, B * D], F32)
-        recip_w = sbuf.tile([P, ROWS, B * D], F32)
-        o_sb = sbuf.tile([P, ROWS, B * D], F32)
+        num = [
+            psum.tile([P, B * D], F32, tag="bank%d" % (4 + s), name="num%d" % s)
+            for s in range(ROWS)
+        ]
         for s in range(ROWS):
-            num_s = psum.tile([P, B * D], F32, tag="bank%d" % (4 + s), name="num%d" % s)
-            nc.tensor.matmul_mx(
-                out=num_s[:],
-                lhsT=eb_codes[:, s * P : (s + 1) * P].bitcast(FP8X4),
-                lhsT_scale=eb_scales[:, s * P : (s + 1) * P],
-                rhs=ekv_codes[:].bitcast(FP8X4),
-                rhs_scale=ekv_scales[:],
-                start=True,
-                stop=True,
-            )
+            mx_product(num[s], s, ekv_codes, ekv_scales)
+        for s in range(ROWS):
             nc.scalar.activation(out=rsqrt_w[:, s, :], in_=w_sb[:, s, :], func=ACT.Abs_reciprocal_sqrt)
             nc.scalar.activation(out=recip_w[:, s, :], in_=rsqrt_w[:, s, :], func=ACT.Square)
-            nc.vector.tensor_tensor(out=o_sb[:, s, :], in0=num_s[:], in1=recip_w[:, s, :], op=ALU.mult)
+            nc.vector.tensor_tensor(out=o_sb[:, s, :], in0=num[s][:], in1=recip_w[:, s, :], op=ALU.mult)
             nc.sync.dma_start(
                 out=out_view[:, s], in_=o_sb[:, s, :].rearrange("p (b d) -> p b d", b=B)
             )

@@ -131,8 +131,8 @@ def tile_modelnew_s_kernel(tc, q, k, v, bias, out):
 
         nc.sync.dma_start(out=bias_sb[:, 0:2, :], in_=bias_view[:, 0:2, :])
         nc.sync.dma_start(out=k_sb[:], in_=k_view)
-        nc.sync.dma_start(out=q_sb[:], in_=q_view)
         nc.sync.dma_start(out=bias_sb[:, 2:4, :], in_=bias_view[:, 2:4, :])
+        nc.sync.dma_start(out=q_sb[:], in_=q_view)
         nc.sync.dma_start(out=v_sb[:], in_=v_view)
 
         make_identity(nc, ident[:])
@@ -144,20 +144,25 @@ def tile_modelnew_s_kernel(tc, q, k, v, bias, out):
         row_exp(0)
         row_exp(1)
         row_transpose(0)
+        row_transpose(1)
+
         nc.vector.tensor_tensor(
             out=k_max2[:], in0=k_sb[:, :, 0:2, :], in1=k_sb[:, :, 2:4, :], op=ALU.max
         )
+        row_max(2)
         nc.vector.tensor_tensor(
             out=k_max1[:], in0=k_max2[:, :, 0, :], in1=k_max2[:, :, 1, :], op=ALU.max
         )
+        row_max(3)
         for b in range(B):
             nc.tensor.transpose(k_maxT[:, b, :], k_max1[:, b, :], ident[:])
-        row_transpose(1)
-        for s in range(ROWS - 1):
-            gate_exp(s)
+        row_exp(2)
+        row_transpose(2)
+        gate_exp(0)
+        gate_exp(1)
+        row_exp(3)
 
-        row_max(2)
-        row_max(3)
+        row_copy(nc.vector.tensor_copy, 0)
         with nc.allow_low_precision(reason="a maximum of bfloat16 values is a bfloat16 value"):
             nc.vector.tensor_reduce(out=mk[:], in_=k_maxT[:], axis=AXIS.X, op=ALU.max)
         for b in range(B):
@@ -168,27 +173,24 @@ def tile_modelnew_s_kernel(tc, q, k, v, bias, out):
                 start=True,
                 stop=True,
             )
-        row_copy(nc.vector.tensor_copy, 0)
-        row_copy(nc.scalar.copy, 1)
-        row_exp(2)
-        row_exp(3)
-        row_transpose(2)
         row_transpose(3)
+        row_copy(nc.vector.tensor_copy, 1)
+        row_copy(nc.scalar.copy, 2)
+        gate_exp(2)
 
         for b in range(B):
             k_subtract(b)
             k_exp(b)
-            if b + 2 < ROWS:
-                row_copy(nc.scalar.copy, b + 2)
-        gate_exp(ROWS - 1)
+        row_copy(nc.scalar.copy, 3)
+        gate_exp(3)
         nc.scalar.activation(out=warm_rsqrt[:], in_=one[:], func=ACT.Abs_reciprocal_sqrt)
 
         ek_round(0)
         ek_round(1)
-        ek_times_v(0)
-        quantise(eb_codes, eb_scales, eb_grouped[:].rearrange("c s p t -> c (s p t)"))
         ek_round(2)
+        ek_times_v(0)
         ek_round(3)
+        quantise(eb_codes, eb_scales, eb_grouped[:].rearrange("c s p t -> c (s p t)"))
         quantise(ek_codes, ek_scales, ek_grouped[:].rearrange("c b d t -> c (b d t)"))
         den = [
             psum.tile([P, B * D], F32, tag="bank%d" % s, name="den%d" % s) for s in range(ROWS)
@@ -216,10 +218,17 @@ def tile_modelnew_s_kernel(tc, q, k, v, bias, out):
         ]
         for s in range(ROWS):
             mx_product(num[s], s, ekv_codes, ekv_scales)
-        for s in range(ROWS):
-            nc.scalar.activation(out=rsqrt_w[:, s, :], in_=w_sb[:, s, :], func=ACT.Abs_reciprocal_sqrt)
-            nc.scalar.activation(out=recip_w[:, s, :], in_=rsqrt_w[:, s, :], func=ACT.Square)
-            nc.vector.tensor_tensor(out=o_sb[:, s, :], in0=num[s][:], in1=recip_w[:, s, :], op=ALU.mult)
-            nc.sync.dma_start(
-                out=out_view[:, s], in_=o_sb[:, s, :].rearrange("p (b d) -> p b d", b=B)
-            )
+        for s in range(ROWS + 1):
+            if s < ROWS:
+                nc.scalar.activation(
+                    out=rsqrt_w[:, s, :], in_=w_sb[:, s, :], func=ACT.Abs_reciprocal_sqrt
+                )
+            if s > 0:
+                r = s - 1
+                nc.scalar.activation(out=recip_w[:, r, :], in_=rsqrt_w[:, r, :], func=ACT.Square)
+                nc.vector.tensor_tensor(
+                    out=o_sb[:, r, :], in0=num[r][:], in1=recip_w[:, r, :], op=ALU.mult
+                )
+                nc.sync.dma_start(
+                    out=out_view[:, r], in_=o_sb[:, r, :].rearrange("p (b d) -> p b d", b=B)
+                )

@@ -129,7 +129,8 @@ def tile_modelnew_s_kernel(tc, q, k, v, bias, out):
                 stop=True,
             )
 
-        nc.sync.dma_start(out=bias_sb[:, 0:2, :], in_=bias_view[:, 0:2, :])
+        nc.sync.dma_start(out=bias_sb[:, 0, :], in_=bias_view[:, 0, :])
+        nc.sync.dma_start(out=bias_sb[:, 1, :], in_=bias_view[:, 1, :])
         nc.sync.dma_start(out=k_sb[:], in_=k_view)
         nc.sync.dma_start(out=bias_sb[:, 2:4, :], in_=bias_view[:, 2:4, :])
         nc.sync.dma_start(out=q_sb[:], in_=q_view)
@@ -198,11 +199,7 @@ def tile_modelnew_s_kernel(tc, q, k, v, bias, out):
         for s in range(ROWS):
             mx_product(den[s], s, ek_codes, ek_scales)
 
-        for s in range(ROWS):
-            if s + 1 < B:
-                ek_times_v(s + 1)
-            else:
-                quantise(ekv_codes, ekv_scales, ekv_grouped[:].rearrange("c b d t -> c (b d t)"))
+        def gated_den(s):
             nc.vector.scalar_tensor_tensor(
                 out=w_sb[:, s, :],
                 in0=e_sb[:, s].rearrange("p b d -> p (b d)"),
@@ -211,6 +208,15 @@ def tile_modelnew_s_kernel(tc, q, k, v, bias, out):
                 op0=ALU.add,
                 op1=ALU.mult,
             )
+
+        ek_times_v(1)
+        ek_times_v(2)
+        gated_den(0)
+        gated_den(1)
+        ek_times_v(3)
+        gated_den(2)
+        quantise(ekv_codes, ekv_scales, ekv_grouped[:].rearrange("c b d t -> c (b d t)"))
+        gated_den(3)
 
         num = [
             psum.tile([P, B * D], F32, tag="bank%d" % (4 + s), name="num%d" % s)
@@ -225,10 +231,18 @@ def tile_modelnew_s_kernel(tc, q, k, v, bias, out):
                 )
             if s > 0:
                 r = s - 1
-                nc.scalar.activation(out=recip_w[:, r, :], in_=rsqrt_w[:, r, :], func=ACT.Square)
-                nc.vector.tensor_tensor(
-                    out=o_sb[:, r, :], in0=num[r][:], in1=recip_w[:, r, :], op=ALU.mult
-                )
-                nc.sync.dma_start(
-                    out=out_view[:, r], in_=o_sb[:, r, :].rearrange("p (b d) -> p b d", b=B)
-                )
+                pieces = 2 if r == ROWS - 1 else 1
+                width = B * D // pieces
+                for piece in range(pieces):
+                    cols = slice(piece * width, (piece + 1) * width)
+                    batches = slice(piece * B // pieces, (piece + 1) * B // pieces)
+                    nc.scalar.activation(
+                        out=recip_w[:, r, cols], in_=rsqrt_w[:, r, cols], func=ACT.Square
+                    )
+                    nc.vector.tensor_tensor(
+                        out=o_sb[:, r, cols], in0=num[r][:, cols], in1=recip_w[:, r, cols], op=ALU.mult
+                    )
+                    nc.sync.dma_start(
+                        out=out_view[:, r, batches],
+                        in_=o_sb[:, r, cols].rearrange("p (b d) -> p b d", d=D),
+                    )

@@ -35,15 +35,17 @@ def tile_modelnew_s_kernel(tc, q, k, v, bias, out):
         out_view = out.rearrange("b (p s) d -> p s b d", s=ROWS)
 
         ident = sbuf.tile([P, P], BF16)
+        ident_f32 = sbuf.tile([P, P], F32)
         one = sbuf.tile([P, 1], F32)
         warm_exp = sbuf.tile([P, 1], F32)
         warm_rsqrt = sbuf.tile([P, 1], F32)
 
         neg_mb = sbuf.tile([P, ROWS], F32)
-        eb_sb = sbuf.tile([P, ROWS, PACK, P], BF16)
+        neg_bias = sbuf.tile([P, ROWS, N], BF16)
+        eb_sb = sbuf.tile([P, ROWS, 2, 2 * P], BF16)
         eb_grouped = sbuf.tile([P, ROWS, P, PACK], BF16, align_bytes=64)
         ebT = [
-            psum.tile([P, PACK, P], BF16, tag="bank%d" % s, name="ebT%d" % s) for s in range(ROWS)
+            psum.tile([P, 2, P], F32, tag="bank%d" % s, name="ebT%d" % s) for s in range(ROWS)
         ]
 
         k_max2 = sbuf.tile([P, B, 2, D], BF16)
@@ -70,25 +72,33 @@ def tile_modelnew_s_kernel(tc, q, k, v, bias, out):
         o_sb = sbuf.tile([P, ROWS, B * D], F32)
 
         def row_max(s):
-            nc.vector.tensor_reduce(
-                out=neg_mb[:, s : s + 1], in_=bias_sb[:, s, :], axis=AXIS.X, op=ALU.max, negate=True
+            nc.vector.tensor_scalar(
+                out=neg_bias[:, s, :],
+                in0=bias_sb[:, s, :],
+                scalar1=-1.0,
+                scalar2=None,
+                op0=ALU.mult,
+                op1=ALU.min,
+                accum_out=neg_mb[:, s : s + 1],
             )
 
         def row_exp(s):
             nc.scalar.activation(
-                out=eb_sb[:, s, :, :],
-                in_=bias_sb[:, s, :].rearrange("p (c t) -> p t c", t=PACK),
+                out=eb_sb[:, s].rearrange("p u (c e) -> p u c e", e=2),
+                in_=bias_sb[:, s, :].rearrange("p (c u e) -> p u c e", u=2, e=2),
                 func=ACT.Exp,
                 bias=neg_mb[:, s : s + 1],
                 scale=1.0,
             )
 
         def row_transpose(s):
-            for t in range(PACK):
-                nc.tensor.transpose(ebT[s][:, t, :], eb_sb[:, s, t, :], ident[:])
+            for u in range(2):
+                nc.tensor.transpose(ebT[s][:, u, :], eb_sb[:, s, u, :].bitcast(F32), ident_f32[:])
 
         def row_copy(engine_copy, s):
-            engine_copy(out=eb_grouped[:, s], in_=ebT[s][:].rearrange("c t p -> c p t"))
+            engine_copy(
+                out=eb_grouped[:, s].bitcast(F32), in_=ebT[s][:].rearrange("c u p -> c p u")
+            )
 
         def gate_exp(s):
             nc.scalar.activation(out=e_sb[:, s], in_=q_sb[:, :, s, :], func=ACT.Exp, scale=-1.0)
@@ -136,6 +146,7 @@ def tile_modelnew_s_kernel(tc, q, k, v, bias, out):
         nc.sync.dma_start(out=q_sb[:], in_=q_view)
         nc.sync.dma_start(out=v_sb[:], in_=v_view)
 
+        make_identity(nc, ident_f32[:])
         make_identity(nc, ident[:])
         nc.vector.memset(one[:], 1.0)
         nc.scalar.activation(out=warm_exp[:], in_=one[:], func=ACT.Exp)

@@ -70,6 +70,8 @@ def tile_modelnew_s_kernel(tc, q, k, v, bias, out):
         rsqrt_w = sbuf.tile([P, ROWS, B * D], F32)
         recip_w = sbuf.tile([P, ROWS, B * D], F32)
         o_sb = sbuf.tile([P, ROWS, B * D], F32)
+        sig_sb = sbuf.tile([P, 2, B * D], F32)
+        g_sb = sbuf.tile([P, 2, B * D], F32)
 
         def row_max(s):
             nc.vector.tensor_scalar(
@@ -102,6 +104,17 @@ def tile_modelnew_s_kernel(tc, q, k, v, bias, out):
 
         def gate_exp(s):
             nc.scalar.activation(out=e_sb[:, s], in_=q_sb[:, :, s, :], func=ACT.Exp, scale=-1.0)
+
+        def gate_sigmoid(s):
+            nc.scalar.activation(out=e_sb[:, s], in_=q_sb[:, :, s, :], func=ACT.Tanh, scale=0.5)
+            nc.gpsimd.tensor_scalar(
+                out=sig_sb[:, s, :],
+                in0=e_sb[:, s].rearrange("p b d -> p (b d)"),
+                scalar1=0.5,
+                scalar2=0.5,
+                op0=ALU.mult,
+                op1=ALU.add,
+            )
 
         def k_subtract(b):
             nc.vector.tensor_tensor(
@@ -170,8 +183,8 @@ def tile_modelnew_s_kernel(tc, q, k, v, bias, out):
             nc.tensor.transpose(k_maxT[:, b, :], k_max1[:, b, :], ident[:])
         row_exp(2)
         row_transpose(2)
-        gate_exp(0)
-        gate_exp(1)
+        gate_sigmoid(0)
+        gate_sigmoid(1)
         row_exp(3)
 
         row_copy(nc.vector.tensor_copy, 0)
@@ -220,11 +233,37 @@ def tile_modelnew_s_kernel(tc, q, k, v, bias, out):
                 op1=ALU.mult,
             )
 
+        def root(s, positive):
+            nc.scalar.activation(
+                out=rsqrt_w[:, s, :], in_=positive, func=ACT.Abs_reciprocal_sqrt
+            )
+
+        def square(s, cols):
+            nc.scalar.activation(out=recip_w[:, s, cols], in_=rsqrt_w[:, s, cols], func=ACT.Square)
+
+        def finish(s, cols, batches, factor):
+            nc.vector.tensor_tensor(
+                out=o_sb[:, s, cols], in0=num[s][:, cols], in1=factor, op=ALU.mult
+            )
+            nc.sync.dma_start(
+                out=out_view[:, s, batches],
+                in_=o_sb[:, s, cols].rearrange("p (b d) -> p b d", d=D),
+            )
+
+        whole = slice(0, B * D)
+        every_batch = slice(0, B)
+
         ek_times_v(1)
         ek_times_v(2)
-        gated_den(0)
-        gated_den(1)
         ek_times_v(3)
+        root(0, den[0][:])
+        root(1, den[1][:])
+        square(0, whole)
+        square(1, whole)
+        for s in range(2):
+            nc.gpsimd.tensor_tensor(
+                out=g_sb[:, s, :], in0=recip_w[:, s, :], in1=sig_sb[:, s, :], op=ALU.mult
+            )
         gated_den(2)
         quantise(ekv_codes, ekv_scales, ekv_grouped[:].rearrange("c b d t -> c (b d t)"))
         gated_den(3)
@@ -235,25 +274,13 @@ def tile_modelnew_s_kernel(tc, q, k, v, bias, out):
         ]
         for s in range(ROWS):
             mx_product(num[s], s, ekv_codes, ekv_scales)
-        for s in range(ROWS + 1):
-            if s < ROWS:
-                nc.scalar.activation(
-                    out=rsqrt_w[:, s, :], in_=w_sb[:, s, :], func=ACT.Abs_reciprocal_sqrt
-                )
-            if s > 0:
-                r = s - 1
-                pieces = 2 if r == ROWS - 1 else 1
-                width = B * D // pieces
-                for piece in range(pieces):
-                    cols = slice(piece * width, (piece + 1) * width)
-                    batches = slice(piece * B // pieces, (piece + 1) * B // pieces)
-                    nc.scalar.activation(
-                        out=recip_w[:, r, cols], in_=rsqrt_w[:, r, cols], func=ACT.Square
-                    )
-                    nc.vector.tensor_tensor(
-                        out=o_sb[:, r, cols], in0=num[r][:, cols], in1=recip_w[:, r, cols], op=ALU.mult
-                    )
-                    nc.sync.dma_start(
-                        out=out_view[:, r, batches],
-                        in_=o_sb[:, r, cols].rearrange("p (b d) -> p b d", d=D),
-                    )
+        root(2, w_sb[:, 2, :])
+        root(3, w_sb[:, 3, :])
+        finish(0, whole, every_batch, g_sb[:, 0, :])
+        finish(1, whole, every_batch, g_sb[:, 1, :])
+        square(2, whole)
+        finish(2, whole, every_batch, recip_w[:, 2, :])
+        for piece in range(2):
+            cols = slice(piece * B * D // 2, (piece + 1) * B * D // 2)
+            square(3, cols)
+            finish(3, cols, slice(piece * B // 2, (piece + 1) * B // 2), recip_w[:, 3, cols])

@@ -50,9 +50,15 @@ def tile_modelnew_s_kernel(tc, q, k, v, bias, out):
 
         k_max2 = sbuf.tile([P, B, 2, D], BF16)
         k_max1 = sbuf.tile([P, B, D], BF16)
-        k_maxT = psum.tile([P, B, P], BF16, tag="bank4")
-        mk = sbuf.tile([P, B], BF16)
-        mk_all = psum.tile([P, B, D], F32, tag="bank5")
+        k_maxT = [
+            psum.tile([P, 2, P], BF16, tag="bank%d" % (4 + 2 * h), name="k_maxT%d" % h)
+            for h in range(2)
+        ]
+        mk = [sbuf.tile([P, 2], BF16, name="mk%d" % h) for h in range(2)]
+        mk_all = [
+            psum.tile([P, 2, D], F32, tag="bank%d" % (5 + 2 * h), name="mk_all%d" % h)
+            for h in range(2)
+        ]
         k_diff = sbuf.tile([P, B, D, PACK], F32)
         ek_f32 = sbuf.tile([P, B, D, PACK], F32)
         ek_grouped = sbuf.tile([P, B, D, PACK], BF16, align_bytes=64)
@@ -66,12 +72,12 @@ def tile_modelnew_s_kernel(tc, q, k, v, bias, out):
         ekv_scales = sbuf.tile([P, B * D], U8, align_bytes=64)
 
         e_sb = sbuf.tile([P, ROWS, B, D], F32)
+        sig_sb = sbuf.tile([P, 2, B * D], F32)
+        g_sb = sbuf.tile([P, 2, B * D], F32)
         w_sb = sbuf.tile([P, ROWS, B * D], F32)
         rsqrt_w = sbuf.tile([P, ROWS, B * D], F32)
         recip_w = sbuf.tile([P, ROWS, B * D], F32)
         o_sb = sbuf.tile([P, ROWS, B * D], F32)
-        sig_sb = sbuf.tile([P, 2, B * D], F32)
-        g_sb = sbuf.tile([P, 2, B * D], F32)
 
         def row_max(s):
             nc.vector.tensor_scalar(
@@ -97,16 +103,18 @@ def tile_modelnew_s_kernel(tc, q, k, v, bias, out):
             for u in range(2):
                 nc.tensor.transpose(ebT[s][:, u, :], eb_sb[:, s, u, :].bitcast(F32), ident_f32[:])
 
-        def row_copy(engine_copy, s):
-            engine_copy(
+        def row_copy(s):
+            nc.vector.tensor_copy(
                 out=eb_grouped[:, s].bitcast(F32), in_=ebT[s][:].rearrange("c u p -> c p u")
             )
 
         def gate_exp(s):
             nc.scalar.activation(out=e_sb[:, s], in_=q_sb[:, :, s, :], func=ACT.Exp, scale=-1.0)
 
-        def gate_sigmoid(s):
+        def gate_tanh(s):
             nc.scalar.activation(out=e_sb[:, s], in_=q_sb[:, :, s, :], func=ACT.Tanh, scale=0.5)
+
+        def gate_sigmoid(s):
             nc.gpsimd.tensor_scalar(
                 out=sig_sb[:, s, :],
                 in0=e_sb[:, s].rearrange("p b d -> p (b d)"),
@@ -116,19 +124,66 @@ def tile_modelnew_s_kernel(tc, q, k, v, bias, out):
                 op1=ALU.add,
             )
 
+        def half(h):
+            return slice(2 * h, 2 * h + 2)
+
+        def k_max_of_pairs(h):
+            nc.vector.tensor_tensor(
+                out=k_max2[:, half(h)],
+                in0=k_sb[:, half(h), 0:2, :],
+                in1=k_sb[:, half(h), 2:4, :],
+                op=ALU.max,
+            )
+
+        def k_max_of_rows(h):
+            nc.vector.tensor_tensor(
+                out=k_max1[:, half(h)],
+                in0=k_max2[:, half(h), 0, :],
+                in1=k_max2[:, half(h), 1, :],
+                op=ALU.max,
+            )
+
+        def k_max_transpose(h):
+            for i in range(2):
+                nc.tensor.transpose(k_maxT[h][:, i, :], k_max1[:, 2 * h + i, :], ident[:])
+
+        def k_max_of_partitions(h):
+            with nc.allow_low_precision(reason="a maximum of bfloat16 values is a bfloat16 value"):
+                nc.vector.tensor_reduce(out=mk[h][:], in_=k_maxT[h][:], axis=AXIS.X, op=ALU.max)
+
+        def k_max_spread(h):
+            for i in range(2):
+                nc.tensor.matmul(
+                    out=mk_all[h][:, i, :],
+                    lhsT=mk[h][:, i : i + 1].to_broadcast([P, P]),
+                    rhs=ident[:],
+                    start=True,
+                    stop=True,
+                )
+
         def k_subtract(b):
             nc.vector.tensor_tensor(
                 out=k_diff[:, b],
                 in0=k_sb[:, b].rearrange("c t d -> c d t"),
-                in1=mk_all[:, b, :].unsqueeze(2).to_broadcast([P, D, PACK]),
+                in1=mk_all[b // 2][:, b % 2, :].unsqueeze(2).to_broadcast([P, D, PACK]),
                 op=ALU.subtract,
             )
 
         def k_exp(b):
             nc.scalar.activation(out=ek_f32[:, b], in_=k_diff[:, b], func=ACT.Exp)
 
-        def ek_round(b):
+        def ek_round_vector(b):
             nc.vector.tensor_copy(out=ek_grouped[:, b], in_=ek_f32[:, b])
+
+        def ek_round_gpsimd(b):
+            nc.gpsimd.tensor_scalar(
+                out=ek_grouped[:, b].rearrange("c d t -> c (d t)"),
+                in0=ek_f32[:, b].rearrange("c d t -> c (d t)"),
+                scalar1=1.0,
+                scalar2=0.0,
+                op0=ALU.mult,
+                op1=ALU.add,
+            )
 
         def ek_times_v(b):
             nc.vector.tensor_tensor(
@@ -154,8 +209,10 @@ def tile_modelnew_s_kernel(tc, q, k, v, bias, out):
 
         nc.sync.dma_start(out=bias_sb[:, 0, :], in_=bias_view[:, 0, :])
         nc.sync.dma_start(out=bias_sb[:, 1, :], in_=bias_view[:, 1, :])
-        nc.sync.dma_start(out=k_sb[:], in_=k_view)
-        nc.sync.dma_start(out=bias_sb[:, 2:4, :], in_=bias_view[:, 2:4, :])
+        nc.sync.dma_start(out=bias_sb[:, 2, :], in_=bias_view[:, 2, :])
+        nc.sync.dma_start(out=k_sb[:, half(0)], in_=k_view[:, half(0)])
+        nc.sync.dma_start(out=bias_sb[:, 3, :], in_=bias_view[:, 3, :])
+        nc.sync.dma_start(out=k_sb[:, half(1)], in_=k_view[:, half(1)])
         nc.sync.dma_start(out=q_sb[:], in_=q_view)
         nc.sync.dma_start(out=v_sb[:], in_=v_view)
 
@@ -166,61 +223,53 @@ def tile_modelnew_s_kernel(tc, q, k, v, bias, out):
 
         row_max(0)
         row_max(1)
+        row_max(2)
         row_exp(0)
         row_exp(1)
+        row_exp(2)
         row_transpose(0)
         row_transpose(1)
-
-        nc.vector.tensor_tensor(
-            out=k_max2[:], in0=k_sb[:, :, 0:2, :], in1=k_sb[:, :, 2:4, :], op=ALU.max
-        )
-        row_max(2)
-        nc.vector.tensor_tensor(
-            out=k_max1[:], in0=k_max2[:, :, 0, :], in1=k_max2[:, :, 1, :], op=ALU.max
-        )
+        k_max_of_pairs(0)
         row_max(3)
-        for b in range(B):
-            nc.tensor.transpose(k_maxT[:, b, :], k_max1[:, b, :], ident[:])
-        row_exp(2)
+        row_exp(3)
+        k_max_of_rows(0)
+        k_max_transpose(0)
         row_transpose(2)
+        k_max_of_pairs(1)
+        row_copy(0)
+        k_max_of_rows(1)
+        k_max_transpose(1)
+        row_transpose(3)
+        row_copy(1)
+        k_max_of_partitions(0)
+        k_max_spread(0)
+        row_copy(2)
+        k_max_of_partitions(1)
+        k_max_spread(1)
+        row_copy(3)
+
+        gate_tanh(0)
+        gate_tanh(1)
         gate_sigmoid(0)
         gate_sigmoid(1)
-        row_exp(3)
-
-        row_copy(nc.vector.tensor_copy, 0)
-        with nc.allow_low_precision(reason="a maximum of bfloat16 values is a bfloat16 value"):
-            nc.vector.tensor_reduce(out=mk[:], in_=k_maxT[:], axis=AXIS.X, op=ALU.max)
-        for b in range(B):
-            nc.tensor.matmul(
-                out=mk_all[:, b, :],
-                lhsT=mk[:, b : b + 1].to_broadcast([P, P]),
-                rhs=ident[:],
-                start=True,
-                stop=True,
-            )
-        row_transpose(3)
-        row_copy(nc.vector.tensor_copy, 1)
-        row_copy(nc.scalar.copy, 2)
         gate_exp(2)
 
         for b in range(B):
             k_subtract(b)
             k_exp(b)
-        row_copy(nc.scalar.copy, 3)
+        for b in range(B - 1):
+            ek_round_gpsimd(b)
         gate_exp(3)
         nc.scalar.activation(out=warm_rsqrt[:], in_=one[:], func=ACT.Abs_reciprocal_sqrt)
 
-        ek_round(0)
-        ek_round(1)
-        ek_round(2)
-        ek_times_v(0)
-        ek_round(3)
         quantise(eb_codes, eb_scales, eb_grouped[:].rearrange("c s p t -> c (s p t)"))
+        ek_round_vector(B - 1)
+        ek_times_v(0)
         quantise(ek_codes, ek_scales, ek_grouped[:].rearrange("c b d t -> c (b d t)"))
         den = [
             psum.tile([P, B * D], F32, tag="bank%d" % s, name="den%d" % s) for s in range(ROWS)
         ]
-        for s in range(ROWS):
+        for s in (0, 2, 1, 3):
             mx_product(den[s], s, ek_codes, ek_scales)
 
         def gated_den(s):
@@ -233,13 +282,18 @@ def tile_modelnew_s_kernel(tc, q, k, v, bias, out):
                 op1=ALU.mult,
             )
 
-        def root(s, positive):
+        def root(s, cols, positive):
             nc.scalar.activation(
-                out=rsqrt_w[:, s, :], in_=positive, func=ACT.Abs_reciprocal_sqrt
+                out=rsqrt_w[:, s, cols], in_=positive, func=ACT.Abs_reciprocal_sqrt
             )
 
         def square(s, cols):
             nc.scalar.activation(out=recip_w[:, s, cols], in_=rsqrt_w[:, s, cols], func=ACT.Square)
+
+        def gate_over_den(s, cols):
+            nc.gpsimd.tensor_tensor(
+                out=g_sb[:, s, cols], in0=recip_w[:, s, cols], in1=sig_sb[:, s, cols], op=ALU.mult
+            )
 
         def finish(s, cols, batches, factor):
             nc.vector.tensor_tensor(
@@ -252,35 +306,41 @@ def tile_modelnew_s_kernel(tc, q, k, v, bias, out):
 
         whole = slice(0, B * D)
         every_batch = slice(0, B)
+        left = slice(0, B * D // 2)
+        right = slice(B * D // 2, B * D)
 
         ek_times_v(1)
         ek_times_v(2)
         ek_times_v(3)
-        root(0, den[0][:])
-        root(1, den[1][:])
-        square(0, whole)
-        square(1, whole)
-        for s in range(2):
-            nc.gpsimd.tensor_tensor(
-                out=g_sb[:, s, :], in0=recip_w[:, s, :], in1=sig_sb[:, s, :], op=ALU.mult
-            )
+        root(0, left, den[0][:, left])
+        root(0, right, den[0][:, right])
+        square(0, left)
+        square(0, right)
+        gate_over_den(0, left)
+        gate_over_den(0, right)
         gated_den(2)
         quantise(ekv_codes, ekv_scales, ekv_grouped[:].rearrange("c b d t -> c (b d t)"))
         gated_den(3)
+        root(1, left, den[1][:, left])
+        root(1, right, den[1][:, right])
+        root(2, whole, w_sb[:, 2, :])
+        square(1, left)
+        square(1, right)
+        gate_over_den(1, left)
+        gate_over_den(1, right)
+        root(3, whole, w_sb[:, 3, :])
+        square(2, whole)
 
         num = [
             psum.tile([P, B * D], F32, tag="bank%d" % (4 + s), name="num%d" % s)
             for s in range(ROWS)
         ]
-        for s in range(ROWS):
+        for s in (0, 2, 1, 3):
             mx_product(num[s], s, ekv_codes, ekv_scales)
-        root(2, w_sb[:, 2, :])
-        root(3, w_sb[:, 3, :])
         finish(0, whole, every_batch, g_sb[:, 0, :])
-        finish(1, whole, every_batch, g_sb[:, 1, :])
-        square(2, whole)
         finish(2, whole, every_batch, recip_w[:, 2, :])
-        for piece in range(2):
-            cols = slice(piece * B * D // 2, (piece + 1) * B * D // 2)
-            square(3, cols)
-            finish(3, cols, slice(piece * B // 2, (piece + 1) * B // 2), recip_w[:, 3, cols])
+        finish(1, whole, every_batch, g_sb[:, 1, :])
+        square(3, left)
+        finish(3, left, slice(0, B // 2), recip_w[:, 3, left])
+        square(3, right)
+        finish(3, right, slice(B // 2, B), recip_w[:, 3, right])

@@ -175,16 +175,6 @@ def tile_modelnew_s_kernel(tc, q, k, v, bias, out):
         def ek_round_vector(b):
             nc.vector.tensor_copy(out=ek_grouped[:, b], in_=ek_f32[:, b])
 
-        def ek_round_gpsimd(b):
-            nc.gpsimd.tensor_scalar(
-                out=ek_grouped[:, b].rearrange("c d t -> c (d t)"),
-                in0=ek_f32[:, b].rearrange("c d t -> c (d t)"),
-                scalar1=1.0,
-                scalar2=0.0,
-                op0=ALU.mult,
-                op1=ALU.add,
-            )
-
         def ek_times_v(b):
             nc.vector.tensor_tensor(
                 out=ekv_grouped[:, b],
@@ -257,14 +247,12 @@ def tile_modelnew_s_kernel(tc, q, k, v, bias, out):
         for b in range(B):
             k_subtract(b)
             k_exp(b)
-        for b in range(B - 1):
-            ek_round_gpsimd(b)
         gate_exp(3)
         nc.scalar.activation(out=warm_rsqrt[:], in_=one[:], func=ACT.Abs_reciprocal_sqrt)
 
+        for b in range(B):
+            ek_round_vector(b)
         quantise(eb_codes, eb_scales, eb_grouped[:].rearrange("c s p t -> c (s p t)"))
-        ek_round_vector(B - 1)
-        ek_times_v(0)
         quantise(ek_codes, ek_scales, ek_grouped[:].rearrange("c b d t -> c (b d t)"))
         den = [
             psum.tile([P, B * D], F32, tag="bank%d" % s, name="den%d" % s) for s in range(ROWS)
@@ -309,9 +297,8 @@ def tile_modelnew_s_kernel(tc, q, k, v, bias, out):
         left = slice(0, B * D // 2)
         right = slice(B * D // 2, B * D)
 
-        ek_times_v(1)
-        ek_times_v(2)
-        ek_times_v(3)
+        for b in range(B):
+            ek_times_v(b)
         root(0, left, den[0][:, left])
         root(0, right, den[0][:, right])
         square(0, left)

@@ -45,22 +45,20 @@ def tile_modelnew_s_kernel(tc, q, k, v, bias, out):
         eb_sb = sbuf.tile([P, ROWS, 2, 2 * P], BF16)
         eb_grouped = sbuf.tile([P, ROWS, P, PACK], BF16, align_bytes=64)
         ebT = [
-            psum.tile([P, 2, P], F32, tag="bank%d" % s, name="ebT%d" % s) for s in range(ROWS)
+            psum.tile([P, 2, 2, P], F32, tag="bank%d" % h, name="ebT%d" % h) for h in range(2)
         ]
 
-        k_max2 = sbuf.tile([P, B, 2, D], BF16)
-        k_max1 = sbuf.tile([P, B, D], BF16)
-        k_maxT = [
-            psum.tile([P, 2, P], BF16, tag="bank%d" % (4 + 2 * h), name="k_maxT%d" % h)
+        kT = [
+            psum.tile([P, 2, PACK * P], BF16, tag="bank%d" % (2 + h), name="kT%d" % h)
             for h in range(2)
         ]
-        mk = [sbuf.tile([P, 2], BF16, name="mk%d" % h) for h in range(2)]
-        mk_all = [
-            psum.tile([P, 2, D], F32, tag="bank%d" % (5 + 2 * h), name="mk_all%d" % h)
-            for h in range(2)
+        neg_k = sbuf.tile([P, B, PACK * P], BF16)
+        neg_mk = sbuf.tile([P, B], F32)
+        ekT = sbuf.tile([P, B, PACK, P], F32)
+        ek_ps = [
+            psum.tile([P, PACK, D], F32, tag="bank%d" % (4 + b), name="ek_ps%d" % b)
+            for b in range(B)
         ]
-        k_diff = sbuf.tile([P, B, D, PACK], F32)
-        ek_f32 = sbuf.tile([P, B, D, PACK], F32)
         ek_grouped = sbuf.tile([P, B, D, PACK], BF16, align_bytes=64)
         ekv_grouped = sbuf.tile([P, B, D, PACK], BF16, align_bytes=64)
 
@@ -101,11 +99,14 @@ def tile_modelnew_s_kernel(tc, q, k, v, bias, out):
 
         def row_transpose(s):
             for u in range(2):
-                nc.tensor.transpose(ebT[s][:, u, :], eb_sb[:, s, u, :].bitcast(F32), ident_f32[:])
+                nc.tensor.transpose(
+                    ebT[s // 2][:, s % 2, u, :], eb_sb[:, s, u, :].bitcast(F32), ident_f32[:]
+                )
 
         def row_copy(s):
             nc.vector.tensor_copy(
-                out=eb_grouped[:, s].bitcast(F32), in_=ebT[s][:].rearrange("c u p -> c p u")
+                out=eb_grouped[:, s].bitcast(F32),
+                in_=ebT[s // 2][:, s % 2].rearrange("c u p -> c p u"),
             )
 
         def gate_exp(s):
@@ -124,61 +125,45 @@ def tile_modelnew_s_kernel(tc, q, k, v, bias, out):
                 op1=ALU.add,
             )
 
-        def half(h):
-            return slice(2 * h, 2 * h + 2)
-
-        def k_max_of_pairs(h):
-            nc.vector.tensor_tensor(
-                out=k_max2[:, half(h)],
-                in0=k_sb[:, half(h), 0:2, :],
-                in1=k_sb[:, half(h), 2:4, :],
-                op=ALU.max,
-            )
-
-        def k_max_of_rows(h):
-            nc.vector.tensor_tensor(
-                out=k_max1[:, half(h)],
-                in0=k_max2[:, half(h), 0, :],
-                in1=k_max2[:, half(h), 1, :],
-                op=ALU.max,
-            )
-
-        def k_max_transpose(h):
-            for i in range(2):
-                nc.tensor.transpose(k_maxT[h][:, i, :], k_max1[:, 2 * h + i, :], ident[:])
-
-        def k_max_of_partitions(h):
-            with nc.allow_low_precision(reason="a maximum of bfloat16 values is a bfloat16 value"):
-                nc.vector.tensor_reduce(out=mk[h][:], in_=k_maxT[h][:], axis=AXIS.X, op=ALU.max)
-
-        def k_max_spread(h):
-            for i in range(2):
-                nc.tensor.matmul(
-                    out=mk_all[h][:, i, :],
-                    lhsT=mk[h][:, i : i + 1].to_broadcast([P, P]),
-                    rhs=ident[:],
-                    start=True,
-                    stop=True,
+        def k_transpose(b):
+            for t in range(PACK):
+                nc.tensor.transpose(
+                    kT[b // 2][:, b % 2, t * P : (t + 1) * P], k_sb[:, b, t, :], ident[:]
                 )
 
-        def k_subtract(b):
-            nc.vector.tensor_tensor(
-                out=k_diff[:, b],
-                in0=k_sb[:, b].rearrange("c t d -> c d t"),
-                in1=mk_all[b // 2][:, b % 2, :].unsqueeze(2).to_broadcast([P, D, PACK]),
-                op=ALU.subtract,
+        def k_max(b):
+            nc.vector.tensor_scalar(
+                out=neg_k[:, b, :],
+                in0=kT[b // 2][:, b % 2, :],
+                scalar1=-1.0,
+                scalar2=None,
+                op0=ALU.mult,
+                op1=ALU.min,
+                accum_out=neg_mk[:, b : b + 1],
             )
 
         def k_exp(b):
-            nc.scalar.activation(out=ek_f32[:, b], in_=k_diff[:, b], func=ACT.Exp)
+            nc.scalar.activation(
+                out=ekT[:, b].rearrange("d t c -> d (t c)"),
+                in_=kT[b // 2][:, b % 2, :],
+                func=ACT.Exp,
+                bias=neg_mk[:, b : b + 1],
+                scale=1.0,
+            )
+
+        def ek_transpose(b):
+            for t in range(PACK):
+                nc.tensor.transpose(ek_ps[b][:, t, :], ekT[:, b, t, :], ident_f32[:])
 
         def ek_round_vector(b):
-            nc.vector.tensor_copy(out=ek_grouped[:, b], in_=ek_f32[:, b])
+            nc.vector.tensor_copy(
+                out=ek_grouped[:, b], in_=ek_ps[b][:].rearrange("c t d -> c d t")
+            )
 
         def ek_times_v(b):
             nc.vector.tensor_tensor(
                 out=ekv_grouped[:, b],
-                in0=ek_f32[:, b],
+                in0=ek_ps[b][:].rearrange("c t d -> c d t"),
                 in1=v_sb[:, b].rearrange("c t d -> c d t"),
                 op=ALU.mult,
             )
@@ -199,10 +184,12 @@ def tile_modelnew_s_kernel(tc, q, k, v, bias, out):
 
         nc.sync.dma_start(out=bias_sb[:, 0, :], in_=bias_view[:, 0, :])
         nc.sync.dma_start(out=bias_sb[:, 1, :], in_=bias_view[:, 1, :])
+        nc.sync.dma_start(out=k_sb[:, 0], in_=k_view[:, 0])
+        nc.sync.dma_start(out=k_sb[:, 1], in_=k_view[:, 1])
         nc.sync.dma_start(out=bias_sb[:, 2, :], in_=bias_view[:, 2, :])
-        nc.sync.dma_start(out=k_sb[:, half(0)], in_=k_view[:, half(0)])
         nc.sync.dma_start(out=bias_sb[:, 3, :], in_=bias_view[:, 3, :])
-        nc.sync.dma_start(out=k_sb[:, half(1)], in_=k_view[:, half(1)])
+        nc.sync.dma_start(out=k_sb[:, 2], in_=k_view[:, 2])
+        nc.sync.dma_start(out=k_sb[:, 3], in_=k_view[:, 3])
         nc.sync.dma_start(out=q_sb[:], in_=q_view)
         nc.sync.dma_start(out=v_sb[:], in_=v_view)
 
@@ -213,40 +200,39 @@ def tile_modelnew_s_kernel(tc, q, k, v, bias, out):
 
         row_max(0)
         row_max(1)
-        row_max(2)
         row_exp(0)
         row_exp(1)
-        row_exp(2)
+        k_transpose(0)
+        k_transpose(1)
         row_transpose(0)
         row_transpose(1)
-        k_max_of_pairs(0)
+        row_max(2)
+        k_max(0)
         row_max(3)
+        k_max(1)
+        row_exp(2)
         row_exp(3)
-        k_max_of_rows(0)
-        k_max_transpose(0)
+        k_exp(0)
+        k_exp(1)
+        k_transpose(2)
+        k_transpose(3)
         row_transpose(2)
-        k_max_of_pairs(1)
-        row_copy(0)
-        k_max_of_rows(1)
-        k_max_transpose(1)
         row_transpose(3)
+        row_copy(0)
         row_copy(1)
-        k_max_of_partitions(0)
-        k_max_spread(0)
+        k_max(2)
+        k_max(3)
+        k_exp(2)
+        k_exp(3)
         row_copy(2)
-        k_max_of_partitions(1)
-        k_max_spread(1)
         row_copy(3)
-
+        for b in range(B):
+            ek_transpose(b)
         gate_tanh(0)
         gate_tanh(1)
         gate_sigmoid(0)
         gate_sigmoid(1)
         gate_exp(2)
-
-        for b in range(B):
-            k_subtract(b)
-            k_exp(b)
         gate_exp(3)
         nc.scalar.activation(out=warm_rsqrt[:], in_=one[:], func=ACT.Abs_reciprocal_sqrt)
 

@@ -243,7 +243,7 @@ def tile_modelnew_s_kernel(tc, q, k, v, bias, out):
         den = [
             psum.tile([P, B * D], F32, tag="bank%d" % s, name="den%d" % s) for s in range(ROWS)
         ]
-        for s in (0, 2, 1, 3):
+        for s in range(ROWS):
             mx_product(den[s], s, ek_codes, ek_scales)
 
         def gated_den(s):
@@ -283,26 +283,23 @@ def tile_modelnew_s_kernel(tc, q, k, v, bias, out):
         left = slice(0, B * D // 2)
         right = slice(B * D // 2, B * D)
 
+        def reciprocal(s, positive):
+            root(s, left, positive[:, left])
+            root(s, right, positive[:, right])
+            square(s, left)
+            square(s, right)
+
         for b in range(B):
             ek_times_v(b)
-        root(0, left, den[0][:, left])
-        root(0, right, den[0][:, right])
-        square(0, left)
-        square(0, right)
-        gate_over_den(0, left)
-        gate_over_den(0, right)
+        for s in range(2):
+            reciprocal(s, den[s])
+            gate_over_den(s, left)
+            gate_over_den(s, right)
         gated_den(2)
         quantise(ekv_codes, ekv_scales, ekv_grouped[:].rearrange("c b d t -> c (b d t)"))
         gated_den(3)
-        root(1, left, den[1][:, left])
-        root(1, right, den[1][:, right])
-        root(2, whole, w_sb[:, 2, :])
-        square(1, left)
-        square(1, right)
-        gate_over_den(1, left)
-        gate_over_den(1, right)
-        root(3, whole, w_sb[:, 3, :])
-        square(2, whole)
+        reciprocal(2, w_sb[:, 2])
+        reciprocal(3, w_sb[:, 3])
 
         num = [
             psum.tile([P, B * D], F32, tag="bank%d" % (4 + s), name="num%d" % s)
@@ -313,7 +310,5 @@ def tile_modelnew_s_kernel(tc, q, k, v, bias, out):
         finish(0, whole, every_batch, g_sb[:, 0, :])
         finish(2, whole, every_batch, recip_w[:, 2, :])
         finish(1, whole, every_batch, g_sb[:, 1, :])
-        square(3, left)
         finish(3, left, slice(0, B // 2), recip_w[:, 3, left])
-        square(3, right)
         finish(3, right, slice(B // 2, B), recip_w[:, 3, right])

@@ -38,7 +38,6 @@ def tile_modelnew_s_kernel(tc, q, k, v, bias, out):
         ident_f32 = sbuf.tile([P, P], F32)
         one = sbuf.tile([P, 1], F32)
         warm_exp = sbuf.tile([P, 1], F32)
-        warm_rsqrt = sbuf.tile([P, 1], F32)
 
         neg_mb = sbuf.tile([P, ROWS], F32)
         neg_bias = sbuf.tile([P, ROWS, N], BF16)
@@ -49,17 +48,12 @@ def tile_modelnew_s_kernel(tc, q, k, v, bias, out):
         ]
 
         kT = [
-            psum.tile([P, 2, PACK * P], BF16, tag="bank%d" % (2 + h), name="kT%d" % h)
-            for h in range(2)
+            psum.tile([P, PACK * P], BF16, tag="bank%d" % (4 + b), name="kT%d" % b) for b in range(B)
         ]
         neg_k = sbuf.tile([P, B, PACK * P], BF16)
         neg_mk = sbuf.tile([P, B], F32)
         ekT = sbuf.tile([P, B, PACK, P], F32)
-        ek_ps = [
-            psum.tile([P, PACK, D], F32, tag="bank%d" % (4 + b), name="ek_ps%d" % b)
-            for b in range(B)
-        ]
-        ek_grouped = sbuf.tile([P, B, D, PACK], BF16, align_bytes=64)
+        ek_grouped = sbuf.tile([P, B, D, PACK], BF16, tag="ek_then_sigmoid", align_bytes=64)
         ekv_grouped = sbuf.tile([P, B, D, PACK], BF16, align_bytes=64)
 
         eb_codes = sbuf.tile([P, ROWS * P], U32, align_bytes=64)
@@ -70,7 +64,6 @@ def tile_modelnew_s_kernel(tc, q, k, v, bias, out):
         ekv_scales = sbuf.tile([P, B * D], U8, align_bytes=64)
 
         e_sb = sbuf.tile([P, ROWS, B, D], F32)
-        sig_sb = sbuf.tile([P, 2, B * D], F32)
         g_sb = sbuf.tile([P, 2, B * D], F32)
         w_sb = sbuf.tile([P, ROWS, B * D], F32)
         rsqrt_w = sbuf.tile([P, ROWS, B * D], F32)
@@ -103,14 +96,19 @@ def tile_modelnew_s_kernel(tc, q, k, v, bias, out):
                     ebT[s // 2][:, s % 2, u, :], eb_sb[:, s, u, :].bitcast(F32), ident_f32[:]
                 )
 
-        def row_copy(s):
+        def row_copy(h):
             nc.vector.tensor_copy(
-                out=eb_grouped[:, s].bitcast(F32),
-                in_=ebT[s // 2][:, s % 2].rearrange("c u p -> c p u"),
+                out=eb_grouped[:, 2 * h : 2 * h + 2].bitcast(F32),
+                in_=ebT[h][:].rearrange("c s u p -> c s p u"),
             )
 
-        def gate_exp(s):
-            nc.scalar.activation(out=e_sb[:, s], in_=q_sb[:, :, s, :], func=ACT.Exp, scale=-1.0)
+        def gate_exp():
+            nc.scalar.activation(
+                out=e_sb[:, 2:4].rearrange("p s b d -> p b s d"),
+                in_=q_sb[:, :, 2:4, :],
+                func=ACT.Exp,
+                scale=-1.0,
+            )
 
         def gate_tanh(s):
             nc.scalar.activation(out=e_sb[:, s], in_=q_sb[:, :, s, :], func=ACT.Tanh, scale=0.5)
@@ -127,14 +125,12 @@ def tile_modelnew_s_kernel(tc, q, k, v, bias, out):
 
         def k_transpose(b):
             for t in range(PACK):
-                nc.tensor.transpose(
-                    kT[b // 2][:, b % 2, t * P : (t + 1) * P], k_sb[:, b, t, :], ident[:]
-                )
+                nc.tensor.transpose(kT[b][:, t * P : (t + 1) * P], k_sb[:, b, t, :], ident[:])
 
         def k_max(b):
             nc.vector.tensor_scalar(
                 out=neg_k[:, b, :],
-                in0=kT[b // 2][:, b % 2, :],
+                in0=kT[b][:],
                 scalar1=-1.0,
                 scalar2=None,
                 op0=ALU.mult,
@@ -145,7 +141,7 @@ def tile_modelnew_s_kernel(tc, q, k, v, bias, out):
         def k_exp(b):
             nc.scalar.activation(
                 out=ekT[:, b].rearrange("d t c -> d (t c)"),
-                in_=kT[b // 2][:, b % 2, :],
+                in_=kT[b][:],
                 func=ACT.Exp,
                 bias=neg_mk[:, b : b + 1],
                 scale=1.0,
@@ -182,14 +178,9 @@ def tile_modelnew_s_kernel(tc, q, k, v, bias, out):
                 stop=True,
             )
 
-        nc.sync.dma_start(out=bias_sb[:, 0, :], in_=bias_view[:, 0, :])
-        nc.sync.dma_start(out=bias_sb[:, 1, :], in_=bias_view[:, 1, :])
-        nc.sync.dma_start(out=k_sb[:, 0], in_=k_view[:, 0])
-        nc.sync.dma_start(out=k_sb[:, 1], in_=k_view[:, 1])
-        nc.sync.dma_start(out=bias_sb[:, 2, :], in_=bias_view[:, 2, :])
-        nc.sync.dma_start(out=bias_sb[:, 3, :], in_=bias_view[:, 3, :])
-        nc.sync.dma_start(out=k_sb[:, 2], in_=k_view[:, 2])
-        nc.sync.dma_start(out=k_sb[:, 3], in_=k_view[:, 3])
+        for i in range(B):
+            nc.sync.dma_start(out=bias_sb[:, i, :], in_=bias_view[:, i, :])
+            nc.sync.dma_start(out=k_sb[:, i], in_=k_view[:, i])
         nc.sync.dma_start(out=q_sb[:], in_=q_view)
         nc.sync.dma_start(out=v_sb[:], in_=v_view)
 
@@ -198,48 +189,55 @@ def tile_modelnew_s_kernel(tc, q, k, v, bias, out):
         nc.vector.memset(one[:], 1.0)
         nc.scalar.activation(out=warm_exp[:], in_=one[:], func=ACT.Exp)
 
+        ek_ps = []
+
+        def ek_back(b):
+            ek_ps.append(psum.tile([P, PACK, D], F32, tag="bank%d" % (4 + b), name="ek_ps%d" % b))
+            ek_transpose(b)
+
         row_max(0)
-        row_max(1)
         row_exp(0)
-        row_exp(1)
         k_transpose(0)
+        row_max(1)
+        row_exp(1)
         k_transpose(1)
+        k_max(0)
+        k_exp(0)
+        row_max(2)
+        row_exp(2)
+        k_transpose(2)
+        k_max(1)
+        k_exp(1)
+        row_max(3)
+        row_exp(3)
+        k_transpose(3)
         row_transpose(0)
         row_transpose(1)
-        row_max(2)
-        k_max(0)
-        row_max(3)
-        k_max(1)
-        row_exp(2)
-        row_exp(3)
-        k_exp(0)
-        k_exp(1)
-        k_transpose(2)
-        k_transpose(3)
-        row_transpose(2)
-        row_transpose(3)
-        row_copy(0)
-        row_copy(1)
+        ek_back(0)
         k_max(2)
-        k_max(3)
         k_exp(2)
+        row_transpose(2)
+        ek_back(1)
+        k_max(3)
         k_exp(3)
-        row_copy(2)
-        row_copy(3)
-        for b in range(B):
-            ek_transpose(b)
+        row_transpose(3)
+        ek_back(2)
+        ek_back(3)
         gate_tanh(0)
         gate_tanh(1)
-        gate_sigmoid(0)
-        gate_sigmoid(1)
-        gate_exp(2)
-        gate_exp(3)
-        nc.scalar.activation(out=warm_rsqrt[:], in_=one[:], func=ACT.Abs_reciprocal_sqrt)
+        gate_exp()
 
-        for b in range(B):
-            ek_round_vector(b)
+        row_copy(0)
+        ek_round_vector(0)
+        ek_round_vector(1)
+        row_copy(1)
+        ek_round_vector(2)
+        ek_round_vector(3)
         quantise(eb_codes, eb_scales, eb_grouped[:].rearrange("c s p t -> c (s p t)"))
         quantise(ek_codes, ek_scales, ek_grouped[:].rearrange("c b d t -> c (b d t)"))
+        sig_sb = sbuf.tile([P, 2, B * D], F32, tag="ek_then_sigmoid", align_bytes=64)
+        gate_sigmoid(0)
+        gate_sigmoid(1)
         den = [
             psum.tile([P, B * D], F32, tag="bank%d" % s, name="den%d" % s) for s in range(ROWS)
         ]

@@ -189,6 +189,12 @@ def tile_modelnew_s_kernel(tc, q, k, v, bias, out):
         nc.vector.memset(one[:], 1.0)
         nc.scalar.activation(out=warm_exp[:], in_=one[:], func=ACT.Exp)
 
+        warm_ps = psum.tile([P, PACK, P], F32, tag="bank2")
+        for i in range(2 * PACK):
+            nc.tensor.matmul(
+                out=warm_ps[:, i % PACK, :], lhsT=ident[:], rhs=ident[:], start=True, stop=True
+            )
+
         ek_ps = []
 
         def ek_back(b):

@@ -37,6 +37,7 @@ def tile_modelnew_s_kernel(tc, q, k, v, bias, out):
         ident = sbuf.tile([P, P], BF16)
         ident_f32 = sbuf.tile([P, P], F32)
         one = sbuf.tile([P, 1], F32)
+        zeros = sbuf.tile([P, P], F32)
         warm_exp = sbuf.tile([P, 1], F32)
 
         neg_mb = sbuf.tile([P, ROWS], F32)
@@ -184,16 +185,21 @@ def tile_modelnew_s_kernel(tc, q, k, v, bias, out):
         nc.sync.dma_start(out=q_sb[:], in_=q_view)
         nc.sync.dma_start(out=v_sb[:], in_=v_view)
 
+        nc.vector.memset(zeros[:], 0.0)
         make_identity(nc, ident_f32[:])
         make_identity(nc, ident[:])
         nc.vector.memset(one[:], 1.0)
         nc.scalar.activation(out=warm_exp[:], in_=one[:], func=ACT.Exp)
 
         warm_ps = psum.tile([P, PACK, P], F32, tag="bank2")
-        for i in range(2 * PACK):
+
+        def keep_warm(i, operand):
             nc.tensor.matmul(
-                out=warm_ps[:, i % PACK, :], lhsT=ident[:], rhs=ident[:], start=True, stop=True
+                out=warm_ps[:, i % PACK, :], lhsT=operand, rhs=operand, start=True, stop=True
             )
+
+        for i in range(4):
+            keep_warm(i, zeros[:])
 
         ek_ps = []
 
@@ -207,6 +213,7 @@ def tile_modelnew_s_kernel(tc, q, k, v, bias, out):
         row_max(1)
         row_exp(1)
         k_transpose(1)
+        keep_warm(0, zeros[:])
         k_max(0)
         k_exp(0)
         row_max(2)
@@ -217,21 +224,28 @@ def tile_modelnew_s_kernel(tc, q, k, v, bias, out):
         row_max(3)
         row_exp(3)
         k_transpose(3)
+        keep_warm(1, zeros[:])
         row_transpose(0)
         row_transpose(1)
+        keep_warm(2, zeros[:])
         ek_back(0)
         k_max(2)
         k_exp(2)
         row_transpose(2)
+        keep_warm(3, zeros[:])
         ek_back(1)
         k_max(3)
         k_exp(3)
         row_transpose(3)
+        keep_warm(0, zeros[:])
         ek_back(2)
         ek_back(3)
         gate_tanh(0)
         gate_tanh(1)
         gate_exp()
+        keep_warm(1, e_sb[:, 0, 0, :])
+        keep_warm(2, e_sb[:, 1, 0, :])
+        keep_warm(3, e_sb[:, 2, 0, :])
 
         row_copy(0)
         ek_round_vector(0)

@@ -14,6 +14,7 @@ P = 128
 PACK = 4
 B, N, D = 4, 512, 128
 ROWS = N // P
+W = ROWS * D
 FLOPS = 2 * 2 * B * N * N * D
 
 
@@ -32,7 +33,7 @@ def tile_modelnew_s_kernel(tc, q, k, v, bias, out):
         v_view = v.rearrange("b (c t) d -> c b t d", t=PACK)
         q_view = q.rearrange("b (p s) d -> p b s d", s=ROWS)
         bias_view = bias.rearrange("(p s) j -> p s j", s=ROWS)
-        out_view = out.rearrange("b (p s) d -> p s b d", s=ROWS)
+        out_view = out.rearrange("b (p s) d -> p b (s d)", s=ROWS)
 
         ident = sbuf.tile([P, P], BF16)
         ident_f32 = sbuf.tile([P, P], F32)
@@ -64,12 +65,12 @@ def tile_modelnew_s_kernel(tc, q, k, v, bias, out):
         ekv_codes = sbuf.tile([P, B * D], U32, align_bytes=64)
         ekv_scales = sbuf.tile([P, B * D], U8, align_bytes=64)
 
-        e_sb = sbuf.tile([P, ROWS, B, D], F32)
-        g_sb = sbuf.tile([P, 2, B * D], F32)
-        w_sb = sbuf.tile([P, ROWS, B * D], F32)
-        rsqrt_w = sbuf.tile([P, ROWS, B * D], F32)
-        recip_w = sbuf.tile([P, ROWS, B * D], F32)
-        o_sb = sbuf.tile([P, ROWS, B * D], F32)
+        e_sb = sbuf.tile([P, B, W], F32)
+        g_sb = sbuf.tile([P, 2, W], F32)
+        w_sb = sbuf.tile([P, B, W], F32)
+        rsqrt_w = sbuf.tile([P, B, W], F32)
+        recip_w = sbuf.tile([P, B, W], F32)
+        o_sb = sbuf.tile([P, B, W], F32)
 
         def row_max(s):
             nc.vector.tensor_scalar(
@@ -105,19 +106,21 @@ def tile_modelnew_s_kernel(tc, q, k, v, bias, out):
 
         def gate_exp():
             nc.scalar.activation(
-                out=e_sb[:, 2:4].rearrange("p s b d -> p b s d"),
-                in_=q_sb[:, :, 2:4, :],
+                out=e_sb[:, 2:4],
+                in_=q_sb[:, 2:4].rearrange("p b s d -> p b (s d)"),
                 func=ACT.Exp,
                 scale=-1.0,
             )
 
-        def gate_tanh(s):
-            nc.scalar.activation(out=e_sb[:, s], in_=q_sb[:, :, s, :], func=ACT.Tanh, scale=0.5)
+        def gate_tanh(b):
+            nc.scalar.activation(
+                out=e_sb[:, b], in_=q_sb[:, b].rearrange("p s d -> p (s d)"), func=ACT.Tanh, scale=0.5
+            )
 
-        def gate_sigmoid(s):
+        def gate_sigmoid(b):
             nc.gpsimd.tensor_scalar(
-                out=sig_sb[:, s, :],
-                in0=e_sb[:, s].rearrange("p b d -> p (b d)"),
+                out=sig_sb[:, b, :],
+                in0=e_sb[:, b],
                 scalar1=0.5,
                 scalar2=0.5,
                 op0=ALU.mult,
@@ -168,16 +171,19 @@ def tile_modelnew_s_kernel(tc, q, k, v, bias, out):
         def quantise(codes, scales, grouped):
             nc.vector.quantize_mx(out=codes[:].bitcast(FP8X4), scales=scales[:], in_=grouped)
 
-        def mx_product(acc, s, codes, scales):
-            nc.tensor.matmul_mx(
-                out=acc[:],
-                lhsT=eb_codes[:, s * P : (s + 1) * P].bitcast(FP8X4),
-                lhsT_scale=eb_scales[:, s * P : (s + 1) * P],
-                rhs=codes[:].bitcast(FP8X4),
-                rhs_scale=scales[:],
-                start=True,
-                stop=True,
-            )
+        def mx_product(acc, b, codes, scales):
+            batch = slice(b * D, (b + 1) * D)
+            for s in range(ROWS):
+                rows = slice(s * P, (s + 1) * P)
+                nc.tensor.matmul_mx(
+                    out=acc[:, s * D : (s + 1) * D],
+                    lhsT=eb_codes[:, rows].bitcast(FP8X4),
+                    lhsT_scale=eb_scales[:, rows],
+                    rhs=codes[:, batch].bitcast(FP8X4),
+                    rhs_scale=scales[:, batch],
+                    start=True,
+                    stop=True,
+                )
 
         for i in range(B):
             nc.sync.dma_start(out=bias_sb[:, i, :], in_=bias_view[:, i, :])
@@ -243,9 +249,9 @@ def tile_modelnew_s_kernel(tc, q, k, v, bias, out):
         gate_tanh(0)
         gate_tanh(1)
         gate_exp()
-        keep_warm(1, e_sb[:, 0, 0, :])
-        keep_warm(2, e_sb[:, 1, 0, :])
-        keep_warm(3, e_sb[:, 2, 0, :])
+        keep_warm(1, e_sb[:, 0, :P])
+        keep_warm(2, e_sb[:, 1, :P])
+        keep_warm(3, e_sb[:, 2, :P])
 
         row_copy(0)
         ek_round_vector(0)
@@ -255,19 +261,19 @@ def tile_modelnew_s_kernel(tc, q, k, v, bias, out):
         ek_round_vector(3)
         quantise(eb_codes, eb_scales, eb_grouped[:].rearrange("c s p t -> c (s p t)"))
         quantise(ek_codes, ek_scales, ek_grouped[:].rearrange("c b d t -> c (b d t)"))
-        sig_sb = sbuf.tile([P, 2, B * D], F32, tag="ek_then_sigmoid", align_bytes=64)
+        sig_sb = sbuf.tile([P, 2, W], F32, tag="ek_then_sigmoid", align_bytes=64)
         gate_sigmoid(0)
         gate_sigmoid(1)
         den = [
-            psum.tile([P, B * D], F32, tag="bank%d" % s, name="den%d" % s) for s in range(ROWS)
+            psum.tile([P, W], F32, tag="bank%d" % b, name="den%d" % b) for b in range(B)
         ]
-        for s in range(ROWS):
-            mx_product(den[s], s, ek_codes, ek_scales)
+        for b in range(B):
+            mx_product(den[b], b, ek_codes, ek_scales)
 
         def gated_den(s):
             nc.vector.scalar_tensor_tensor(
                 out=w_sb[:, s, :],
-                in0=e_sb[:, s].rearrange("p b d -> p (b d)"),
+                in0=e_sb[:, s],
                 scalar=1.0,
                 in1=den[s][:],
                 op0=ALU.add,
@@ -287,19 +293,18 @@ def tile_modelnew_s_kernel(tc, q, k, v, bias, out):
                 out=g_sb[:, s, cols], in0=recip_w[:, s, cols], in1=sig_sb[:, s, cols], op=ALU.mult
             )
 
-        def finish(s, cols, batches, factor):
+        def finish(s, cols, factor):
             nc.vector.tensor_tensor(
                 out=o_sb[:, s, cols], in0=num[s][:, cols], in1=factor, op=ALU.mult
             )
             nc.sync.dma_start(
-                out=out_view[:, s, batches],
-                in_=o_sb[:, s, cols].rearrange("p (b d) -> p b d", d=D),
+                out=out_view[:, s, cols],
+                in_=o_sb[:, s, cols],
             )
 
-        whole = slice(0, B * D)
-        every_batch = slice(0, B)
-        left = slice(0, B * D // 2)
-        right = slice(B * D // 2, B * D)
+        whole = slice(0, W)
+        left = slice(0, W // 2)
+        right = slice(W // 2, W)
 
         def reciprocal(s, positive):
             root(s, left, positive[:, left])
@@ -320,13 +325,13 @@ def tile_modelnew_s_kernel(tc, q, k, v, bias, out):
         reciprocal(3, w_sb[:, 3])
 
         num = [
-            psum.tile([P, B * D], F32, tag="bank%d" % (4 + s), name="num%d" % s)
-            for s in range(ROWS)
+            psum.tile([P, W], F32, tag="bank%d" % (4 + b), name="num%d" % b)
+            for b in range(B)
         ]
-        for s in (0, 2, 1, 3):
-            mx_product(num[s], s, ekv_codes, ekv_scales)
-        finish(0, whole, every_batch, g_sb[:, 0, :])
-        finish(2, whole, every_batch, recip_w[:, 2, :])
-        finish(1, whole, every_batch, g_sb[:, 1, :])
-        finish(3, left, slice(0, B // 2), recip_w[:, 3, left])
-        finish(3, right, slice(B // 2, B), recip_w[:, 3, right])
+        for b in (0, 2, 1, 3):
+            mx_product(num[b], b, ekv_codes, ekv_scales)
+        finish(0, whole, g_sb[:, 0, :])
+        finish(2, whole, recip_w[:, 2, :])
+        finish(1, whole, g_sb[:, 1, :])
+        finish(3, left, recip_w[:, 3, left])
+        finish(3, right, recip_w[:, 3, right])

@@ -44,7 +44,9 @@ def tile_modelnew_s_kernel(tc, q, k, v, bias, out):
         neg_mb = sbuf.tile([P, ROWS], F32)
         neg_bias = sbuf.tile([P, ROWS, N], BF16)
         eb_sb = sbuf.tile([P, ROWS, 2, 2 * P], BF16)
-        eb_grouped = sbuf.tile([P, ROWS, P, PACK], BF16, align_bytes=64)
+        eb_grouped = sbuf.tile(
+            [P, ROWS, P, PACK], BF16, tag="eb_then_sigmoid", align_bytes=64
+        )
         ebT = [
             psum.tile([P, 2, 2, P], F32, tag="bank%d" % h, name="ebT%d" % h) for h in range(2)
         ]
@@ -55,7 +57,12 @@ def tile_modelnew_s_kernel(tc, q, k, v, bias, out):
         neg_k = sbuf.tile([P, B, PACK * P], BF16)
         neg_mk = sbuf.tile([P, B], F32)
         ekT = sbuf.tile([P, B, PACK, P], F32)
-        ek_grouped = sbuf.tile([P, B, D, PACK], BF16, tag="ek_then_sigmoid", align_bytes=64)
+        ek_pairs = sbuf.tile([P, B, 2, 2 * P], BF16)
+        ek_words = [
+            psum.tile([P, 2, 2, P], F32, tag="bank%d" % (2 + h), name="ek_words%d" % h)
+            for h in range(2)
+        ]
+        ek_grouped = sbuf.tile([P, B, D, PACK], BF16, align_bytes=64)
         ekv_grouped = sbuf.tile([P, B, D, PACK], BF16, align_bytes=64)
 
         eb_codes = sbuf.tile([P, ROWS * P], U32, align_bytes=64)
@@ -66,7 +73,8 @@ def tile_modelnew_s_kernel(tc, q, k, v, bias, out):
         ekv_scales = sbuf.tile([P, B * D], U8, align_bytes=64)
 
         e_sb = sbuf.tile([P, B, W], F32)
-        g_sb = sbuf.tile([P, 2, W], F32)
+        g_sb = sbuf.tile([P, W], F32)
+        y_sb = sbuf.tile([P, W], F32)
         w_sb = sbuf.tile([P, B, W], F32)
         rsqrt_w = sbuf.tile([P, B, W], F32)
         recip_w = sbuf.tile([P, B, W], F32)
@@ -104,22 +112,25 @@ def tile_modelnew_s_kernel(tc, q, k, v, bias, out):
                 in_=ebT[h][:].rearrange("c s u p -> c s p u"),
             )
 
-        def gate_exp():
+        def gate_exp(batches):
             nc.scalar.activation(
-                out=e_sb[:, 2:4],
-                in_=q_sb[:, 2:4].rearrange("p b s d -> p b (s d)"),
+                out=e_sb[:, batches],
+                in_=q_sb[:, batches].rearrange("p b s d -> p b (s d)"),
                 func=ACT.Exp,
                 scale=-1.0,
             )
 
-        def gate_tanh(b):
+        def gate_tanh(batches):
             nc.scalar.activation(
-                out=e_sb[:, b], in_=q_sb[:, b].rearrange("p s d -> p (s d)"), func=ACT.Tanh, scale=0.5
+                out=e_sb[:, batches],
+                in_=q_sb[:, batches].rearrange("p b s d -> p b (s d)"),
+                func=ACT.Tanh,
+                scale=0.5,
             )
 
         def gate_sigmoid(b):
             nc.gpsimd.tensor_scalar(
-                out=sig_sb[:, b, :],
+                out=sig_sb[:],
                 in0=e_sb[:, b],
                 scalar1=0.5,
                 scalar2=0.5,
@@ -155,9 +166,26 @@ def tile_modelnew_s_kernel(tc, q, k, v, bias, out):
             for t in range(PACK):
                 nc.tensor.transpose(ek_ps[b][:, t, :], ekT[:, b, t, :], ident_f32[:])
 
-        def ek_round_vector(b):
+        def ek_round(b):
+            nc.gpsimd.tensor_scalar(
+                out=ek_pairs[:, b].rearrange("d u (c e) -> d u c e", e=2),
+                in0=ekT[:, b].rearrange("d (u e) c -> d u c e", e=2),
+                scalar1=1.0,
+                scalar2=0.0,
+                op0=ALU.mult,
+                op1=ALU.add,
+            )
+
+        def words_transpose(b):
+            for u in range(2):
+                nc.tensor.transpose(
+                    ek_words[b // 2][:, b % 2, u, :], ek_pairs[:, b, u, :].bitcast(F32), ident_f32[:]
+                )
+
+        def words_copy(h):
             nc.vector.tensor_copy(
-                out=ek_grouped[:, b], in_=ek_ps[b][:].rearrange("c t d -> c d t")
+                out=ek_grouped[:, 2 * h : 2 * h + 2].bitcast(F32),
+                in_=ek_words[h][:].rearrange("c b u d -> c b d u"),
             )
 
         def ek_times_v(b):
@@ -168,8 +196,13 @@ def tile_modelnew_s_kernel(tc, q, k, v, bias, out):
                 op=ALU.mult,
             )
 
-        def quantise(codes, scales, grouped):
-            nc.vector.quantize_mx(out=codes[:].bitcast(FP8X4), scales=scales[:], in_=grouped)
+        def quantise_pair(codes, scales, grouped, h):
+            cols = slice(2 * h * D, (2 * h + 2) * D)
+            nc.vector.quantize_mx(
+                out=codes[:, cols].bitcast(FP8X4),
+                scales=scales[:, cols],
+                in_=grouped[:, 2 * h : 2 * h + 2].rearrange("c b d t -> c (b d t)"),
+            )
 
         def mx_product(acc, b, codes, scales):
             batch = slice(b * D, (b + 1) * D)
@@ -185,11 +218,23 @@ def tile_modelnew_s_kernel(tc, q, k, v, bias, out):
                     stop=True,
                 )
 
-        for i in range(B):
-            nc.sync.dma_start(out=bias_sb[:, i, :], in_=bias_view[:, i, :])
-            nc.sync.dma_start(out=k_sb[:, i], in_=k_view[:, i])
+        def load_bias(s):
+            nc.sync.dma_start(out=bias_sb[:, s, :], in_=bias_view[:, s, :])
+
+        def load_k(b):
+            nc.sync.dma_start(out=k_sb[:, b], in_=k_view[:, b])
+
+        load_bias(0)
+        load_k(0)
+        load_bias(1)
+        load_k(1)
+        load_bias(2)
+        load_bias(3)
+        load_k(2)
+        load_k(3)
+        nc.sync.dma_start(out=v_sb[:, 0:2], in_=v_view[:, 0:2])
         nc.sync.dma_start(out=q_sb[:], in_=q_view)
-        nc.sync.dma_start(out=v_sb[:], in_=v_view)
+        nc.sync.dma_start(out=v_sb[:, 2:4], in_=v_view[:, 2:4])
 
         nc.vector.memset(zeros[:], 0.0)
         make_identity(nc, ident_f32[:])
@@ -197,15 +242,15 @@ def tile_modelnew_s_kernel(tc, q, k, v, bias, out):
         nc.vector.memset(one[:], 1.0)
         nc.scalar.activation(out=warm_exp[:], in_=one[:], func=ACT.Exp)
 
-        warm_ps = psum.tile([P, PACK, P], F32, tag="bank2")
+        warm_ps = ek_words[1][:].rearrange("c b u d -> c (b u) d")
 
-        def keep_warm(i, operand):
+        def keep_warm(i):
             nc.tensor.matmul(
-                out=warm_ps[:, i % PACK, :], lhsT=operand, rhs=operand, start=True, stop=True
+                out=warm_ps[:, i, :], lhsT=zeros[:], rhs=zeros[:], start=True, stop=True
             )
 
-        for i in range(4):
-            keep_warm(i, zeros[:])
+        for i in range(PACK):
+            keep_warm(i)
 
         ek_ps = []
 
@@ -219,119 +264,149 @@ def tile_modelnew_s_kernel(tc, q, k, v, bias, out):
         row_max(1)
         row_exp(1)
         k_transpose(1)
-        keep_warm(0, zeros[:])
+        keep_warm(0)
         k_max(0)
         k_exp(0)
+        ek_round(0)
+        row_transpose(0)
+        k_max(1)
+        k_exp(1)
+        ek_round(1)
+        row_transpose(1)
         row_max(2)
         row_exp(2)
         k_transpose(2)
-        k_max(1)
-        k_exp(1)
         row_max(3)
         row_exp(3)
         k_transpose(3)
-        keep_warm(1, zeros[:])
-        row_transpose(0)
-        row_transpose(1)
-        keep_warm(2, zeros[:])
-        ek_back(0)
+        keep_warm(1)
         k_max(2)
         k_exp(2)
-        row_transpose(2)
-        keep_warm(3, zeros[:])
-        ek_back(1)
+        ek_round(2)
+        ek_back(0)
         k_max(3)
         k_exp(3)
+        ek_round(3)
+        ek_back(1)
+        keep_warm(2)
+        words_transpose(0)
+        row_transpose(2)
         row_transpose(3)
-        keep_warm(0, zeros[:])
+        words_transpose(1)
         ek_back(2)
         ek_back(3)
-        gate_tanh(0)
-        gate_tanh(1)
-        gate_exp()
-        keep_warm(1, e_sb[:, 0, :P])
-        keep_warm(2, e_sb[:, 1, :P])
-        keep_warm(3, e_sb[:, 2, :P])
+        words_transpose(2)
+        words_transpose(3)
+        gate_tanh(slice(0, 2))
+        gate_exp(slice(2, 4))
 
-        row_copy(0)
-        ek_round_vector(0)
-        ek_round_vector(1)
-        row_copy(1)
-        ek_round_vector(2)
-        ek_round_vector(3)
-        quantise(eb_codes, eb_scales, eb_grouped[:].rearrange("c s p t -> c (s p t)"))
-        quantise(ek_codes, ek_scales, ek_grouped[:].rearrange("c b d t -> c (b d t)"))
-        sig_sb = sbuf.tile([P, 2, W], F32, tag="ek_then_sigmoid", align_bytes=64)
-        gate_sigmoid(0)
-        gate_sigmoid(1)
-        den = [
-            psum.tile([P, W], F32, tag="bank%d" % b, name="den%d" % b) for b in range(B)
-        ]
-        for b in range(B):
+        den = []
+        num = []
+
+        def make_den(b):
+            den.append(psum.tile([P, W], F32, tag="bank%d" % b, name="den%d" % b))
             mx_product(den[b], b, ek_codes, ek_scales)
 
-        def gated_den(s):
+        def make_num(b):
+            num.append(psum.tile([P, W], F32, tag="bank%d" % (4 + b), name="num%d" % b))
+            mx_product(num[b], b, ekv_codes, ekv_scales)
+
+        def gated_den(b):
             nc.vector.scalar_tensor_tensor(
-                out=w_sb[:, s, :],
-                in0=e_sb[:, s],
+                out=w_sb[:, b, :],
+                in0=e_sb[:, b],
                 scalar=1.0,
-                in1=den[s][:],
+                in1=den[b][:],
                 op0=ALU.add,
                 op1=ALU.mult,
             )
 
-        def root(s, cols, positive):
-            nc.scalar.activation(
-                out=rsqrt_w[:, s, cols], in_=positive, func=ACT.Abs_reciprocal_sqrt
-            )
-
-        def square(s, cols):
-            nc.scalar.activation(out=recip_w[:, s, cols], in_=rsqrt_w[:, s, cols], func=ACT.Square)
-
-        def gate_over_den(s, cols):
-            nc.gpsimd.tensor_tensor(
-                out=g_sb[:, s, cols], in0=recip_w[:, s, cols], in1=sig_sb[:, s, cols], op=ALU.mult
-            )
-
-        def finish(s, cols, factor):
-            nc.vector.tensor_tensor(
-                out=o_sb[:, s, cols], in0=num[s][:, cols], in1=factor, op=ALU.mult
-            )
-            nc.sync.dma_start(
-                out=out_view[:, s, cols],
-                in_=o_sb[:, s, cols],
+        def gated_num(b):
+            nc.vector.scalar_tensor_tensor(
+                out=y_sb[:],
+                in0=e_sb[:, b],
+                scalar=1.0,
+                in1=num[b][:],
+                op0=ALU.add,
+                op1=ALU.mult,
             )
 
         whole = slice(0, W)
         left = slice(0, W // 2)
         right = slice(W // 2, W)
 
-        def reciprocal(s, positive):
-            root(s, left, positive[:, left])
-            root(s, right, positive[:, right])
-            square(s, left)
-            square(s, right)
+        def reciprocal(b, positive, scale=1.0):
+            for cols in (left, right):
+                nc.scalar.activation(
+                    out=rsqrt_w[:, b, cols],
+                    in_=positive[:, cols],
+                    func=ACT.Abs_reciprocal_sqrt,
+                    scale=scale,
+                )
+            for cols in (left, right):
+                nc.scalar.activation(
+                    out=recip_w[:, b, cols], in_=rsqrt_w[:, b, cols], func=ACT.Square
+                )
 
-        for b in range(B):
-            ek_times_v(b)
-        for s in range(2):
-            reciprocal(s, den[s])
-            gate_over_den(s, left)
-            gate_over_den(s, right)
+        def store(b, cols):
+            nc.sync.dma_start(out=out_view[:, b, cols], in_=o_sb[:, b, cols])
+
+        def gate_over_den(b, cols):
+            nc.gpsimd.tensor_tensor(
+                out=g_sb[:, cols], in0=recip_w[:, b, cols], in1=sig_sb[:, cols], op=ALU.mult
+            )
+
+        def finish(b, cols, factor):
+            nc.vector.tensor_tensor(
+                out=o_sb[:, b, cols], in0=num[b][:, cols], in1=factor, op=ALU.mult
+            )
+            store(b, cols)
+
+        def finish_gpsimd(b, cols):
+            nc.gpsimd.tensor_tensor(
+                out=o_sb[:, b, cols], in0=y_sb[:, cols], in1=recip_w[:, b, cols], op=ALU.mult
+            )
+            store(b, cols)
+
+        row_copy(0)
+        ek_times_v(0)
+        ek_times_v(1)
+        words_copy(0)
+        row_copy(1)
+        quantise_pair(ek_codes, ek_scales, ek_grouped, 0)
+        nc.vector.quantize_mx(
+            out=eb_codes[:].bitcast(FP8X4),
+            scales=eb_scales[:],
+            in_=eb_grouped[:].rearrange("c s p t -> c (s p t)"),
+        )
+        sig_sb = sbuf.tile([P, W], F32, tag="eb_then_sigmoid", align_bytes=64)
+        gate_sigmoid(0)
+        make_den(0)
+        make_den(1)
+        words_copy(1)
+        quantise_pair(ekv_codes, ekv_scales, ekv_grouped, 0)
+        make_num(0)
+        make_num(1)
+        reciprocal(0, den[0])
+        gate_over_den(0, left)
+        gate_over_den(0, right)
+        reciprocal(1, den[1], scale=2.0)
+        ek_times_v(2)
+        quantise_pair(ek_codes, ek_scales, ek_grouped, 1)
+        make_den(2)
+        make_den(3)
+        ek_times_v(3)
+        gated_num(1)
         gated_den(2)
-        quantise(ekv_codes, ekv_scales, ekv_grouped[:].rearrange("c b d t -> c (b d t)"))
-        gated_den(3)
         reciprocal(2, w_sb[:, 2])
+        quantise_pair(ekv_codes, ekv_scales, ekv_grouped, 1)
+        make_num(2)
+        make_num(3)
+        gated_den(3)
         reciprocal(3, w_sb[:, 3])
-
-        num = [
-            psum.tile([P, W], F32, tag="bank%d" % (4 + b), name="num%d" % b)
-            for b in range(B)
-        ]
-        for b in (0, 2, 1, 3):
-            mx_product(num[b], b, ekv_codes, ekv_scales)
-        finish(0, whole, g_sb[:, 0, :])
-        finish(2, whole, recip_w[:, 2, :])
-        finish(1, whole, g_sb[:, 1, :])
+        finish(0, whole, g_sb[:])
+        finish_gpsimd(1, left)
+        finish_gpsimd(1, right)
+        finish(2, whole, recip_w[:, 2])
         finish(3, left, recip_w[:, 3, left])
         finish(3, right, recip_w[:, 3, right])

@@ -57,11 +57,8 @@ def tile_modelnew_s_kernel(tc, q, k, v, bias, out):
         neg_k = sbuf.tile([P, B, PACK * P], BF16)
         neg_mk = sbuf.tile([P, B], F32)
         ekT = sbuf.tile([P, B, PACK, P], F32)
-        ek_pairs = sbuf.tile([P, B, 2, 2 * P], BF16)
-        ek_words = [
-            psum.tile([P, 2, 2, P], F32, tag="bank%d" % (2 + h), name="ek_words%d" % h)
-            for h in range(2)
-        ]
+        ek_pairs = sbuf.tile([P, 2, 2, 2 * P], BF16)
+        ek_words = psum.tile([P, 2, 2, P], F32, tag="bank2")
         ek_grouped = sbuf.tile([P, B, D, PACK], BF16, align_bytes=64)
         ekv_grouped = sbuf.tile([P, B, D, PACK], BF16, align_bytes=64)
 
@@ -94,10 +91,10 @@ def tile_modelnew_s_kernel(tc, q, k, v, bias, out):
         def row_exp(s):
             nc.scalar.activation(
                 out=eb_sb[:, s].rearrange("p u (c e) -> p u c e", e=2),
-                in_=bias_sb[:, s, :].rearrange("p (c u e) -> p u c e", u=2, e=2),
+                in_=neg_bias[:, s, :].rearrange("p (c u e) -> p u c e", u=2, e=2),
                 func=ACT.Exp,
                 bias=neg_mb[:, s : s + 1],
-                scale=1.0,
+                scale=-1.0,
             )
 
         def row_transpose(s):
@@ -120,12 +117,9 @@ def tile_modelnew_s_kernel(tc, q, k, v, bias, out):
                 scale=-1.0,
             )
 
-        def gate_tanh(batches):
+        def gate_tanh(b):
             nc.scalar.activation(
-                out=e_sb[:, batches],
-                in_=q_sb[:, batches].rearrange("p b s d -> p b (s d)"),
-                func=ACT.Tanh,
-                scale=0.5,
+                out=e_sb[:, b], in_=q_sb[:, b].rearrange("p s d -> p (s d)"), func=ACT.Tanh, scale=0.5
             )
 
         def gate_sigmoid(b):
@@ -156,19 +150,24 @@ def tile_modelnew_s_kernel(tc, q, k, v, bias, out):
         def k_exp(b):
             nc.scalar.activation(
                 out=ekT[:, b].rearrange("d t c -> d (t c)"),
-                in_=kT[b][:],
+                in_=neg_k[:, b, :],
                 func=ACT.Exp,
                 bias=neg_mk[:, b : b + 1],
-                scale=1.0,
+                scale=-1.0,
             )
 
         def ek_transpose(b):
             for t in range(PACK):
                 nc.tensor.transpose(ek_ps[b][:, t, :], ekT[:, b, t, :], ident_f32[:])
 
-        def ek_round(b):
+        def ek_round_vector(b):
+            nc.vector.tensor_copy(
+                out=ek_grouped[:, b], in_=ek_ps[b][:].rearrange("c t d -> c d t")
+            )
+
+        def ek_round_gpsimd(b):
             nc.gpsimd.tensor_scalar(
-                out=ek_pairs[:, b].rearrange("d u (c e) -> d u c e", e=2),
+                out=ek_pairs[:, b - 2].rearrange("d u (c e) -> d u c e", e=2),
                 in0=ekT[:, b].rearrange("d (u e) c -> d u c e", e=2),
                 scalar1=1.0,
                 scalar2=0.0,
@@ -179,13 +178,13 @@ def tile_modelnew_s_kernel(tc, q, k, v, bias, out):
         def words_transpose(b):
             for u in range(2):
                 nc.tensor.transpose(
-                    ek_words[b // 2][:, b % 2, u, :], ek_pairs[:, b, u, :].bitcast(F32), ident_f32[:]
+                    ek_words[:, b - 2, u, :], ek_pairs[:, b - 2, u, :].bitcast(F32), ident_f32[:]
                 )
 
-        def words_copy(h):
+        def words_copy():
             nc.vector.tensor_copy(
-                out=ek_grouped[:, 2 * h : 2 * h + 2].bitcast(F32),
-                in_=ek_words[h][:].rearrange("c b u d -> c b d u"),
+                out=ek_grouped[:, 2:4].bitcast(F32),
+                in_=ek_words[:].rearrange("c b u d -> c b d u"),
             )
 
         def ek_times_v(b):
@@ -224,16 +223,11 @@ def tile_modelnew_s_kernel(tc, q, k, v, bias, out):
         def load_k(b):
             nc.sync.dma_start(out=k_sb[:, b], in_=k_view[:, b])
 
-        load_bias(0)
-        load_k(0)
-        load_bias(1)
-        load_k(1)
-        load_bias(2)
-        load_bias(3)
-        load_k(2)
-        load_k(3)
-        nc.sync.dma_start(out=v_sb[:, 0:2], in_=v_view[:, 0:2])
+        for i in range(B):
+            load_bias(i)
+            load_k(i)
         nc.sync.dma_start(out=q_sb[:], in_=q_view)
+        nc.sync.dma_start(out=v_sb[:, 0:2], in_=v_view[:, 0:2])
         nc.sync.dma_start(out=v_sb[:, 2:4], in_=v_view[:, 2:4])
 
         nc.vector.memset(zeros[:], 0.0)
@@ -242,7 +236,7 @@ def tile_modelnew_s_kernel(tc, q, k, v, bias, out):
         nc.vector.memset(one[:], 1.0)
         nc.scalar.activation(out=warm_exp[:], in_=one[:], func=ACT.Exp)
 
-        warm_ps = ek_words[1][:].rearrange("c b u d -> c (b u) d")
+        warm_ps = psum.tile([P, PACK, P], F32, tag="bank3")
 
         def keep_warm(i):
             nc.tensor.matmul(
@@ -267,37 +261,39 @@ def tile_modelnew_s_kernel(tc, q, k, v, bias, out):
         keep_warm(0)
         k_max(0)
         k_exp(0)
-        ek_round(0)
-        row_transpose(0)
-        k_max(1)
-        k_exp(1)
-        ek_round(1)
-        row_transpose(1)
         row_max(2)
         row_exp(2)
         k_transpose(2)
+        k_max(1)
+        k_exp(1)
         row_max(3)
         row_exp(3)
         k_transpose(3)
         keep_warm(1)
+        row_transpose(0)
+        row_transpose(1)
+        keep_warm(2)
+        ek_back(0)
         k_max(2)
         k_exp(2)
-        ek_round(2)
-        ek_back(0)
+        ek_round_gpsimd(2)
+        row_transpose(2)
+        keep_warm(3)
+        ek_back(1)
         k_max(3)
         k_exp(3)
-        ek_round(3)
-        ek_back(1)
-        keep_warm(2)
-        words_transpose(0)
-        row_transpose(2)
+        ek_round_gpsimd(3)
         row_transpose(3)
-        words_transpose(1)
+        keep_warm(0)
         ek_back(2)
         ek_back(3)
+        keep_warm(1)
         words_transpose(2)
+        keep_warm(2)
         words_transpose(3)
-        gate_tanh(slice(0, 2))
+        keep_warm(3)
+        gate_tanh(0)
+        gate_tanh(1)
         gate_exp(slice(2, 4))
 
         den = []
@@ -369,9 +365,10 @@ def tile_modelnew_s_kernel(tc, q, k, v, bias, out):
             store(b, cols)
 
         row_copy(0)
+        ek_round_vector(0)
+        ek_round_vector(1)
         ek_times_v(0)
         ek_times_v(1)
-        words_copy(0)
         row_copy(1)
         quantise_pair(ek_codes, ek_scales, ek_grouped, 0)
         nc.vector.quantize_mx(
@@ -383,7 +380,8 @@ def tile_modelnew_s_kernel(tc, q, k, v, bias, out):
         gate_sigmoid(0)
         make_den(0)
         make_den(1)
-        words_copy(1)
+        ek_times_v(2)
+        words_copy()
         quantise_pair(ekv_codes, ekv_scales, ekv_grouped, 0)
         make_num(0)
         make_num(1)
@@ -391,7 +389,6 @@ def tile_modelnew_s_kernel(tc, q, k, v, bias, out):
         gate_over_den(0, left)
         gate_over_den(0, right)
         reciprocal(1, den[1], scale=2.0)
-        ek_times_v(2)
         quantise_pair(ek_codes, ek_scales, ek_grouped, 1)
         make_den(2)
         make_den(3)
@@ -404,8 +401,9 @@ def tile_modelnew_s_kernel(tc, q, k, v, bias, out):
         make_num(3)
         gated_den(3)
         reciprocal(3, w_sb[:, 3])
-        finish(0, whole, g_sb[:])
+        finish(0, left, g_sb[:, left])
         finish_gpsimd(1, left)
+        finish(0, right, g_sb[:, right])
         finish_gpsimd(1, right)
         finish(2, whole, recip_w[:, 2])
         finish(3, left, recip_w[:, 3, left])

@@ -258,33 +258,29 @@ def tile_modelnew_s_kernel(tc, q, k, v, bias, out):
         row_max(1)
         row_exp(1)
         k_transpose(1)
-        keep_warm(0)
         k_max(0)
         k_exp(0)
         row_max(2)
-        row_exp(2)
-        k_transpose(2)
         k_max(1)
         k_exp(1)
+        row_exp(2)
+        k_transpose(2)
         row_max(3)
-        row_exp(3)
         k_transpose(3)
-        keep_warm(1)
-        row_transpose(0)
-        row_transpose(1)
-        keep_warm(2)
-        ek_back(0)
         k_max(2)
         k_exp(2)
         ek_round_gpsimd(2)
-        row_transpose(2)
-        keep_warm(3)
+        row_exp(3)
+        row_transpose(0)
+        row_transpose(1)
+        ek_back(0)
         ek_back(1)
+        keep_warm(0)
         k_max(3)
         k_exp(3)
         ek_round_gpsimd(3)
+        row_transpose(2)
         row_transpose(3)
-        keep_warm(0)
         ek_back(2)
         ek_back(3)
         keep_warm(1)
@@ -381,7 +377,6 @@ def tile_modelnew_s_kernel(tc, q, k, v, bias, out):
         make_den(0)
         make_den(1)
         ek_times_v(2)
-        words_copy()
         quantise_pair(ekv_codes, ekv_scales, ekv_grouped, 0)
         make_num(0)
         make_num(1)
@@ -389,19 +384,20 @@ def tile_modelnew_s_kernel(tc, q, k, v, bias, out):
         gate_over_den(0, left)
         gate_over_den(0, right)
         reciprocal(1, den[1], scale=2.0)
+        words_copy()
+        ek_times_v(3)
         quantise_pair(ek_codes, ek_scales, ek_grouped, 1)
         make_den(2)
         make_den(3)
-        ek_times_v(3)
         gated_num(1)
         gated_den(2)
         reciprocal(2, w_sb[:, 2])
         quantise_pair(ekv_codes, ekv_scales, ekv_grouped, 1)
         make_num(2)
         make_num(3)
+        finish(0, left, g_sb[:, left])
         gated_den(3)
         reciprocal(3, w_sb[:, 3])
-        finish(0, left, g_sb[:, left])
         finish_gpsimd(1, left)
         finish(0, right, g_sb[:, right])
         finish_gpsimd(1, right)

import concourse.mybir as mybir
from concourse.masks import make_identity

FP8X4 = mybir.dt.float8_e4m3fn_x4
BF16 = mybir.dt.bfloat16
F32 = mybir.dt.float32
U32 = mybir.dt.uint32
U8 = mybir.dt.uint8
ACT = mybir.ActivationFunctionType
ALU = mybir.AluOpType
AXIS = mybir.AxisListType

P = 128
PACK = 4
B, N, D = 4, 512, 128
ROWS = N // P
W = ROWS * D
FLOPS = 2 * 2 * B * N * N * D


def tile_modelnew_s_kernel(tc, q, k, v, bias, out):
    nc = tc.nc
    with (
        tc.tile_pool(name="sbuf", bufs=1) as sbuf,
        tc.psum_pool(name="psum", bufs=1) as psum,
        tc.manual_schedule(),
    ):
        k_sb = sbuf.tile([P, B, PACK, D], BF16)
        v_sb = sbuf.tile([P, B, PACK, D], BF16)
        q_sb = sbuf.tile([P, B, ROWS, D], BF16)
        bias_sb = sbuf.tile([P, ROWS, N], BF16)
        k_view = k.rearrange("b (c t) d -> c b t d", t=PACK)
        v_view = v.rearrange("b (c t) d -> c b t d", t=PACK)
        q_view = q.rearrange("b (p s) d -> p b s d", s=ROWS)
        bias_view = bias.rearrange("(p s) j -> p s j", s=ROWS)
        out_view = out.rearrange("b (p s) d -> p b (s d)", s=ROWS)

        ident = sbuf.tile([P, P], BF16)
        ident_f32 = sbuf.tile([P, P], F32)
        one = sbuf.tile([P, 1], F32)
        zeros = sbuf.tile([P, P], F32)
        warm_exp = sbuf.tile([P, 1], F32)

        neg_mb = sbuf.tile([P, ROWS], F32)
        neg_bias = sbuf.tile([P, ROWS, N], BF16)
        eb_sb = sbuf.tile([P, ROWS, 2, 2 * P], BF16)
        eb_grouped = sbuf.tile(
            [P, ROWS, P, PACK], BF16, tag="eb_then_sigmoid", align_bytes=64
        )
        ebT = [
            psum.tile([P, 2, 2, P], F32, tag="bank%d" % h, name="ebT%d" % h) for h in range(2)
        ]

        kT = [
            psum.tile([P, PACK * P], BF16, tag="bank%d" % (4 + b), name="kT%d" % b) for b in range(B)
        ]
        neg_k = sbuf.tile([P, B, PACK * P], BF16)
        neg_mk = sbuf.tile([P, B], F32)
        ekT = sbuf.tile([P, B, PACK, P], F32)
        ek_pairs = sbuf.tile([P, 2, 2, 2 * P], BF16)
        ek_words = psum.tile([P, 2, 2, P], F32, tag="bank2")
        ek_grouped = sbuf.tile([P, B, D, PACK], BF16, align_bytes=64)
        ekv_grouped = sbuf.tile([P, B, D, PACK], BF16, align_bytes=64)

        eb_codes = sbuf.tile([P, ROWS * P], U32, align_bytes=64)
        eb_scales = sbuf.tile([P, ROWS * P], U8, align_bytes=64)
        ek_codes = sbuf.tile([P, B * D], U32, align_bytes=64)
        ek_scales = sbuf.tile([P, B * D], U8, align_bytes=64)
        ekv_codes = sbuf.tile([P, B * D], U32, align_bytes=64)
        ekv_scales = sbuf.tile([P, B * D], U8, align_bytes=64)

        e_sb = sbuf.tile([P, B, W], F32)
        g_sb = sbuf.tile([P, W], F32)
        y_sb = sbuf.tile([P, W], F32)
        w_sb = sbuf.tile([P, B, W], F32)
        rsqrt_w = sbuf.tile([P, B, W], F32)
        recip_w = sbuf.tile([P, B, W], F32)
        o_sb = sbuf.tile([P, B, W], F32)

        def row_max(s):
            nc.vector.tensor_scalar(
                out=neg_bias[:, s, :],
                in0=bias_sb[:, s, :],
                scalar1=-1.0,
                scalar2=None,
                op0=ALU.mult,
                op1=ALU.min,
                accum_out=neg_mb[:, s : s + 1],
            )

        def row_exp(s):
            nc.scalar.activation(
                out=eb_sb[:, s].rearrange("p u (c e) -> p u c e", e=2),
                in_=neg_bias[:, s, :].rearrange("p (c u e) -> p u c e", u=2, e=2),
                func=ACT.Exp,
                bias=neg_mb[:, s : s + 1],
                scale=-1.0,
            )

        def row_transpose(s):
            for u in range(2):
                nc.tensor.transpose(
                    ebT[s // 2][:, s % 2, u, :], eb_sb[:, s, u, :].bitcast(F32), ident_f32[:]
                )

        def row_copy(h):
            nc.vector.tensor_copy(
                out=eb_grouped[:, 2 * h : 2 * h + 2].bitcast(F32),
                in_=ebT[h][:].rearrange("c s u p -> c s p u"),
            )

        def gate_exp(batches):
            nc.scalar.activation(
                out=e_sb[:, batches],
                in_=q_sb[:, batches].rearrange("p b s d -> p b (s d)"),
                func=ACT.Exp,
                scale=-1.0,
            )

        def gate_tanh(b):
            nc.scalar.activation(
                out=e_sb[:, b], in_=q_sb[:, b].rearrange("p s d -> p (s d)"), func=ACT.Tanh, scale=0.5
            )

        def gate_sigmoid(b):
            nc.gpsimd.tensor_scalar(
                out=sig_sb[:],
                in0=e_sb[:, b],
                scalar1=0.5,
                scalar2=0.5,
                op0=ALU.mult,
                op1=ALU.add,
            )

        def k_transpose(b):
            for t in range(PACK):
                nc.tensor.transpose(kT[b][:, t * P : (t + 1) * P], k_sb[:, b, t, :], ident[:])

        def k_max(b):
            nc.vector.tensor_scalar(
                out=neg_k[:, b, :],
                in0=kT[b][:],
                scalar1=-1.0,
                scalar2=None,
                op0=ALU.mult,
                op1=ALU.min,
                accum_out=neg_mk[:, b : b + 1],
            )

        def k_exp(b):
            nc.scalar.activation(
                out=ekT[:, b].rearrange("d t c -> d (t c)"),
                in_=neg_k[:, b, :],
                func=ACT.Exp,
                bias=neg_mk[:, b : b + 1],
                scale=-1.0,
            )

        def ek_transpose(b):
            for t in range(PACK):
                nc.tensor.transpose(ek_ps[b][:, t, :], ekT[:, b, t, :], ident_f32[:])

        def ek_round_vector(b):
            nc.vector.tensor_copy(
                out=ek_grouped[:, b], in_=ek_ps[b][:].rearrange("c t d -> c d t")
            )

        def ek_round_gpsimd(b):
            nc.gpsimd.tensor_scalar(
                out=ek_pairs[:, b - 2].rearrange("d u (c e) -> d u c e", e=2),
                in0=ekT[:, b].rearrange("d (u e) c -> d u c e", e=2),
                scalar1=1.0,
                scalar2=0.0,
                op0=ALU.mult,
                op1=ALU.add,
            )

        def words_transpose(b):
            for u in range(2):
                nc.tensor.transpose(
                    ek_words[:, b - 2, u, :], ek_pairs[:, b - 2, u, :].bitcast(F32), ident_f32[:]
                )

        def words_copy():
            nc.vector.tensor_copy(
                out=ek_grouped[:, 2:4].bitcast(F32),
                in_=ek_words[:].rearrange("c b u d -> c b d u"),
            )

        def ek_times_v(b):
            nc.vector.tensor_tensor(
                out=ekv_grouped[:, b],
                in0=ek_ps[b][:].rearrange("c t d -> c d t"),
                in1=v_sb[:, b].rearrange("c t d -> c d t"),
                op=ALU.mult,
            )

        def quantise_pair(codes, scales, grouped, h):
            cols = slice(2 * h * D, (2 * h + 2) * D)
            nc.vector.quantize_mx(
                out=codes[:, cols].bitcast(FP8X4),
                scales=scales[:, cols],
                in_=grouped[:, 2 * h : 2 * h + 2].rearrange("c b d t -> c (b d t)"),
            )

        def mx_product(acc, b, codes, scales):
            batch = slice(b * D, (b + 1) * D)
            for s in range(ROWS):
                rows = slice(s * P, (s + 1) * P)
                nc.tensor.matmul_mx(
                    out=acc[:, s * D : (s + 1) * D],
                    lhsT=eb_codes[:, rows].bitcast(FP8X4),
                    lhsT_scale=eb_scales[:, rows],
                    rhs=codes[:, batch].bitcast(FP8X4),
                    rhs_scale=scales[:, batch],
                    start=True,
                    stop=True,
                )

        def load_bias(s):
            nc.sync.dma_start(out=bias_sb[:, s, :], in_=bias_view[:, s, :])

        def load_k(b):
            nc.sync.dma_start(out=k_sb[:, b], in_=k_view[:, b])

        for i in range(B):
            load_bias(i)
            load_k(i)
        nc.sync.dma_start(out=q_sb[:], in_=q_view)
        nc.sync.dma_start(out=v_sb[:, 0:2], in_=v_view[:, 0:2])
        nc.sync.dma_start(out=v_sb[:, 2:4], in_=v_view[:, 2:4])

        nc.vector.memset(zeros[:], 0.0)
        make_identity(nc, ident_f32[:])
        make_identity(nc, ident[:])
        nc.vector.memset(one[:], 1.0)
        nc.scalar.activation(out=warm_exp[:], in_=one[:], func=ACT.Exp)

        warm_ps = psum.tile([P, PACK, P], F32, tag="bank3")

        def keep_warm(i):
            nc.tensor.matmul(
                out=warm_ps[:, i, :], lhsT=zeros[:], rhs=zeros[:], start=True, stop=True
            )

        for i in range(PACK):
            keep_warm(i)

        ek_ps = []

        def ek_back(b):
            ek_ps.append(psum.tile([P, PACK, D], F32, tag="bank%d" % (4 + b), name="ek_ps%d" % b))
            ek_transpose(b)

        row_max(0)
        row_exp(0)
        k_transpose(0)
        row_max(1)
        row_exp(1)
        k_transpose(1)
        k_max(0)
        k_exp(0)
        row_max(2)
        k_max(1)
        k_exp(1)
        row_exp(2)
        k_transpose(2)
        row_max(3)
        k_transpose(3)
        k_max(2)
        k_exp(2)
        ek_round_gpsimd(2)
        row_exp(3)
        row_transpose(0)
        row_transpose(1)
        ek_back(0)
        ek_back(1)
        keep_warm(0)
        k_max(3)
        k_exp(3)
        ek_round_gpsimd(3)
        row_transpose(2)
        row_transpose(3)
        ek_back(2)
        ek_back(3)
        keep_warm(1)
        words_transpose(2)
        keep_warm(2)
        words_transpose(3)
        keep_warm(3)
        gate_tanh(0)
        gate_tanh(1)
        gate_exp(slice(2, 4))

        den = []
        num = []

        def make_den(b):
            den.append(psum.tile([P, W], F32, tag="bank%d" % b, name="den%d" % b))
            mx_product(den[b], b, ek_codes, ek_scales)

        def make_num(b):
            num.append(psum.tile([P, W], F32, tag="bank%d" % (4 + b), name="num%d" % b))
            mx_product(num[b], b, ekv_codes, ekv_scales)

        def gated_den(b):
            nc.vector.scalar_tensor_tensor(
                out=w_sb[:, b, :],
                in0=e_sb[:, b],
                scalar=1.0,
                in1=den[b][:],
                op0=ALU.add,
                op1=ALU.mult,
            )

        def gated_num(b):
            nc.vector.scalar_tensor_tensor(
                out=y_sb[:],
                in0=e_sb[:, b],
                scalar=1.0,
                in1=num[b][:],
                op0=ALU.add,
                op1=ALU.mult,
            )

        whole = slice(0, W)
        left = slice(0, W // 2)
        right = slice(W // 2, W)

        def reciprocal(b, positive, scale=1.0):
            for cols in (left, right):
                nc.scalar.activation(
                    out=rsqrt_w[:, b, cols],
                    in_=positive[:, cols],
                    func=ACT.Abs_reciprocal_sqrt,
                    scale=scale,
                )
            for cols in (left, right):
                nc.scalar.activation(
                    out=recip_w[:, b, cols], in_=rsqrt_w[:, b, cols], func=ACT.Square
                )

        def store(b, cols):
            nc.sync.dma_start(out=out_view[:, b, cols], in_=o_sb[:, b, cols])

        def gate_over_den(b, cols):
            nc.gpsimd.tensor_tensor(
                out=g_sb[:, cols], in0=recip_w[:, b, cols], in1=sig_sb[:, cols], op=ALU.mult
            )

        def finish(b, cols, factor):
            nc.vector.tensor_tensor(
                out=o_sb[:, b, cols], in0=num[b][:, cols], in1=factor, op=ALU.mult
            )
            store(b, cols)

        def finish_gpsimd(b, cols):
            nc.gpsimd.tensor_tensor(
                out=o_sb[:, b, cols], in0=y_sb[:, cols], in1=recip_w[:, b, cols], op=ALU.mult
            )
            store(b, cols)

        row_copy(0)
        ek_round_vector(0)
        ek_round_vector(1)
        ek_times_v(0)
        ek_times_v(1)
        row_copy(1)
        quantise_pair(ek_codes, ek_scales, ek_grouped, 0)
        nc.vector.quantize_mx(
            out=eb_codes[:].bitcast(FP8X4),
            scales=eb_scales[:],
            in_=eb_grouped[:].rearrange("c s p t -> c (s p t)"),
        )
        sig_sb = sbuf.tile([P, W], F32, tag="eb_then_sigmoid", align_bytes=64)
        gate_sigmoid(0)
        make_den(0)
        make_den(1)
        ek_times_v(2)
        quantise_pair(ekv_codes, ekv_scales, ekv_grouped, 0)
        make_num(0)
        make_num(1)
        reciprocal(0, den[0])
        gate_over_den(0, left)
        gate_over_den(0, right)
        reciprocal(1, den[1], scale=2.0)
        words_copy()
        ek_times_v(3)
        quantise_pair(ek_codes, ek_scales, ek_grouped, 1)
        make_den(2)
        make_den(3)
        gated_num(1)
        gated_den(2)
        reciprocal(2, w_sb[:, 2])
        quantise_pair(ekv_codes, ekv_scales, ekv_grouped, 1)
        make_num(2)
        make_num(3)
        finish(0, left, g_sb[:, left])
        gated_den(3)
        reciprocal(3, w_sb[:, 3])
        finish_gpsimd(1, left)
        finish(0, right, g_sb[:, right])
        finish_gpsimd(1, right)
        finish(2, whole, recip_w[:, 2])
        finish(3, left, recip_w[:, 3, left])
        finish(3, right, recip_w[:, 3, right])
